import numpy as np
import ml_dtypes


def mxq(x, axis, fmt="e4m3"):
    dtype, down = {"e4m3": (ml_dtypes.float8_e4m3fn, 7), "e5m2": (ml_dtypes.float8_e5m2, 14)}[fmt]
    v = np.moveaxis(np.asarray(x, np.float32).astype(ml_dtypes.bfloat16).astype(np.float64), axis, -1)
    blocks = v.reshape(v.shape[:-1] + (-1, 32))
    amax = np.abs(blocks).max(-1, keepdims=True)
    byte = np.maximum(np.where(amax > 0, np.frexp(amax)[1] - 1 + 127, 0) - down, 1)
    scale = np.exp2(byte - 127.0)
    codes = (blocks / scale).astype(np.float32).astype(dtype).astype(np.float64)
    return np.moveaxis((codes * scale).reshape(v.shape), -1, axis)


WIDE = False


def mx_kscale(k):
    if not WIDE:
        return np.ones(k)
    levels = np.array([10, -10, 5, -5, 0])
    a = np.random.permutation(np.resize(levels, k // 512 * 4)).reshape(k // 512, 4)
    idx = np.arange(k)
    return np.exp2(a[idx // 512, idx % 128 // 32])


BF16 = ml_dtypes.bfloat16


def bf(x):
    return np.asarray(x, np.float32).astype(BF16)


def f64(x):
    return np.asarray(x).astype(np.float64)


E2M1 = np.array([0.0, 0.5, 1.0, 1.5, 2.0, 3.0, 4.0, 6.0, -0.0, -0.5, -1.0, -1.5, -2.0, -3.0, -4.0, -6.0])


def pack_weight(w, fmt):
    k, n = w.shape
    w = f64(bf(w)).reshape(k // 32, 32, n)
    amax = np.abs(w).max(1)
    if fmt == "e4m3":
        byte = np.frexp(amax)[1] - 1 + 127 - 7
    else:
        mant, ex = np.frexp(amax / 6.0)
        byte = np.where(mant > 0.5, ex, ex - 1) + 127
    byte = np.clip(np.where(amax > 0, byte, 1), 1, 254)
    scaled = (w * np.exp2(127.0 - byte)[:, None, :]).reshape(k, n).astype(np.float32)
    by_word = np.ascontiguousarray(scaled.reshape(k // 512, 128, 4, n).transpose(0, 1, 3, 2))
    if fmt == "e4m3":
        words = by_word.astype(ml_dtypes.float8_e4m3fn).view(np.uint8)
    else:
        c = by_word.astype(ml_dtypes.float4_e2m1fn).view(np.uint8) & 0xF
        words = c[..., 0::2] | (c[..., 1::2] << 4)
    return np.ascontiguousarray(words), np.ascontiguousarray(byte.astype(np.uint8).reshape(k // 512, 16, n))


def unpack_weight(words, scales, fmt):
    g, p, n, _ = words.shape
    if fmt == "e4m3":
        vals = np.ascontiguousarray(words).view(ml_dtypes.float8_e4m3fn).astype(np.float64)
    else:
        nib = np.empty((g, p, n, 4), np.uint8)
        nib[..., 0::2] = words & 0xF
        nib[..., 1::2] = words >> 4
        vals = E2M1[nib]
    vals = vals * np.repeat(np.exp2(scales.astype(np.float64) - 127.0), 8, axis=1)[..., None]
    return vals.transpose(0, 1, 3, 2).reshape(g * 512, n)


B, S, FIN, D, AF, F, H = 4, 128, 128, 8192, 256, 4096, 16
MAX_TIMESCALE = 10000.0
MIN_TIMESCALE = 1.0
EPS = 1e-3


def timing_signal(length, channels):
    num_ts = channels // 2
    log_inc = np.log(MAX_TIMESCALE / MIN_TIMESCALE) / max(num_ts - 1, 1)
    inv_ts = MIN_TIMESCALE * np.exp(np.arange(num_ts) * -log_inc)
    scaled = np.arange(length)[:, None] * inv_ts[None, :]
    return np.concatenate([np.sin(scaled), np.cos(scaled)], axis=1)[None, :, :]


def layer_norm(v, gamma, beta):
    mu = v.mean(-1, keepdims=True)
    var = v.var(-1, keepdims=True)
    return (v - mu) / np.sqrt(var + EPS) * gamma + beta


def setup_inputs():
    r = np.random.standard_normal
    s = mx_kscale(D)
    x = bf(r((B, S, FIN)))
    W_emb = bf(r((FIN, D)) / np.sqrt(FIN))
    b_emb = bf(0.1 * r(D))
    g0 = bf((1.0 + 0.1 * r(D)) * s)
    beta0 = bf(0.1 * r(D) * s)
    Wq_words, Wq_scales = pack_weight(r((D, AF)) / np.sqrt(D) / s[:, None], "e4m3")
    bq = bf(0.1 * r(AF))
    Wk_words, Wk_scales = pack_weight(r((D, AF)) / np.sqrt(D) / s[:, None], "e4m3")
    bk = bf(0.1 * r(AF))
    Wv_words, Wv_scales = pack_weight(r((D, AF)) / np.sqrt(D) / s[:, None], "e4m3")
    bv = bf(0.1 * r(AF))
    return {"x": x,
            "W_emb": W_emb, "b_emb": b_emb,
            "g0": g0, "beta0": beta0,
            "Wq_words": Wq_words, "Wq_scales": Wq_scales, "bq": bq,
            "Wk_words": Wk_words, "Wk_scales": Wk_scales, "bk": bk,
            "Wv_words": Wv_words, "Wv_scales": Wv_scales, "bv": bv}


def reference(x, W_emb, b_emb, g0, beta0, Wq_words, Wq_scales, bq, Wk_words, Wk_scales, bk, Wv_words, Wv_scales, bv):
    h = np.maximum(f64(x) @ f64(W_emb) + f64(b_emb), 0.0)
    h = h + timing_signal(S, D)
    h = layer_norm(h, f64(g0), f64(beta0))
    hq = mxq(h, 2, "e4m3")
    q = (hq @ unpack_weight(Wq_words, Wq_scales, "e4m3")) + f64(bq)
    k = (hq @ unpack_weight(Wk_words, Wk_scales, "e4m3")) + f64(bk)
    v = (hq @ unpack_weight(Wv_words, Wv_scales, "e4m3")) + f64(bv)
    return q, k, v

@@ -1,0 +1,338 @@
+import math
+from contextlib import ExitStack
+
+import concourse.mybir as mybir
+from concourse.masks import make_identity
+
+F32 = mybir.dt.float32
+BF16 = mybir.dt.bfloat16
+I32 = mybir.dt.int32
+U32 = mybir.dt.uint32
+U8 = mybir.dt.uint8
+FP8X4 = mybir.dt.float8_e4m3fn_x4
+ACT = mybir.ActivationFunctionType
+ALU = mybir.AluOpType
+AXIS = mybir.AxisListType
+
+P = 128
+BATCH = 4
+SEQ = 128
+TOKENS = BATCH * SEQ
+D = 8192
+PACK = 4
+K_PASS = P * PACK
+GROUPS = D // K_PASS
+SINE_GROUPS = GROUPS // 2
+N_OUT = 256
+N_ALL = 3 * N_OUT
+N_TILES = N_ALL // P
+EPS = 1e-3
+MAX_TIMESCALE = 10000.0
+
+FLOPS = 2 * TOKENS * P * D + 2 * TOKENS * D * N_ALL
+
+
+def inv_timescale(i):
+    return MAX_TIMESCALE ** (-i / (D // 2 - 1.0))
+
+
+def tile_ffnn_encoder_pa_k_kernel(
+    tc, x, W_emb, b_emb, g0, beta0,
+    Wq_words, Wq_scales, bq, Wk_words, Wk_scales, bk, Wv_words, Wv_scales, bv,
+    out_0, out_1, out_2,
+):
+    nc = tc.nc
+    weights = ((Wq_words, Wq_scales, bq), (Wk_words, Wk_scales, bk), (Wv_words, Wv_scales, bv))
+    outs = (out_0, out_1, out_2)
+
+    with ExitStack() as ctx:
+        keep = ctx.enter_context(tc.tile_pool(name="keep", bufs=1))
+
+        x_rows = keep.tile([P, BATCH, P], BF16)
+        nc.sync.dma_start(out=x_rows[:], in_=x.rearrange("b s f -> s b f"))
+        vec_bf = keep.tile([P, 3, GROUPS, PACK], BF16)
+        for i, vec in enumerate((b_emb, g0, beta0)):
+            nc.sync.dma_start(
+                out=vec_bf[:, i], in_=vec.rearrange("(g m t) -> m g t", g=GROUPS, m=P, t=PACK)
+            )
+        vec_f32 = keep.tile([P, 3, GROUPS * PACK], F32)
+        nc.vector.tensor_copy(out=vec_f32[:], in_=vec_bf[:].rearrange("p v g t -> p v (g t)"))
+        bias_emb, gain, beta = vec_f32[:, 0], vec_f32[:, 1], vec_f32[:, 2]
+
+        w_words = keep.tile([P, GROUPS, N_ALL], U32, align_bytes=64)
+        w_planes = keep.tile([P, GROUPS, N_ALL], U8, align_bytes=64)
+        nc.vector.memset(w_planes[:].rearrange("p g n -> p (g n)").bitcast(I32), 0)
+        bias_rows = keep.tile([P, P], BF16)
+        nc.vector.memset(bias_rows[:], 0.0)
+        for o, (words, scales, bias) in enumerate(weights):
+            cols = slice(o * N_OUT, (o + 1) * N_OUT)
+            nc.sync.dma_start(out=bias_rows[2 * o : 2 * o + 2, :], in_=bias.rearrange("(h n) -> h n", h=2))
+            for quad in range(4):
+                nc.sync.dma_start(
+                    out=w_planes[32 * quad : 32 * quad + 4, :, cols].bitcast(I32),
+                    in_=scales.rearrange("g q n -> q g n")[4 * quad : 4 * quad + 4].bitcast(I32),
+                )
+        for o, (words, scales, bias) in enumerate(weights):
+            cols = slice(o * N_OUT, (o + 1) * N_OUT)
+            nc.sync.dma_start(
+                out=w_words[:, :, cols].bitcast(I32),
+                in_=words.rearrange("g p n t -> p g (n t)").bitcast(I32),
+            )
+
+        ident_f32 = keep.tile([P, P], F32)
+        make_identity(nc, ident_f32[:])
+        ident_bf = keep.tile([P, P], BF16)
+        make_identity(nc, ident_bf[:])
+        pos_i = keep.tile([P, 1], I32)
+        nc.gpsimd.iota(pos_i[:], pattern=[[0, 1]], base=0, channel_multiplier=1)
+        pos_f = keep.tile([P, 1], F32)
+        nc.vector.tensor_copy(out=pos_f[:], in_=pos_i[:])
+        zero_col = keep.tile([P, 1], F32)
+        nc.vector.memset(zero_col[:], 0.0)
+        half_pi = keep.tile([P, 1], F32)
+        nc.vector.tensor_scalar_add(out=half_pi[:], in0=zero_col[:], scalar1=math.pi / 2)
+        eps_col = keep.tile([P, 1], F32)
+        nc.vector.tensor_scalar_add(out=eps_col[:], in0=zero_col[:], scalar1=EPS)
+
+        w_base = keep.tile([P, K_PASS], F32)
+        nc.vector.memset(w_base[:, 0:1], 1.0)
+        for bit in range(7):
+            n = 1 << bit
+            nc.vector.tensor_scalar_mul(
+                out=w_base[:, n : 2 * n], in0=w_base[:, 0:n], scalar1=inv_timescale(PACK * n)
+            )
+        for bit in range(2):
+            n = P << bit
+            nc.vector.tensor_scalar_mul(
+                out=w_base[:, n : 2 * n], in0=w_base[:, 0:n], scalar1=inv_timescale(1 << bit)
+            )
+        pos_w = keep.tile([P, SINE_GROUPS], F32)
+        for j in range(SINE_GROUPS):
+            nc.vector.tensor_scalar_mul(
+                out=pos_w[:, j : j + 1], in0=pos_f[:], scalar1=inv_timescale(K_PASS * j)
+            )
+
+        sum_e = keep.tile([P, BATCH, GROUPS], F32)
+        sq_scalar = keep.tile([P, BATCH, GROUPS // 2], F32)
+        sq_vector = keep.tile([P, BATCH, GROUPS // 2], F32)
+        e_rows = [keep.tile([P, BATCH, K_PASS], F32, name="e_rows%d" % g) for g in range(GROUPS)]
+        xT = keep.tile([P, TOKENS], BF16)
+        bias_col = keep.tile([P, N_TILES], F32)
+
+        with ExitStack() as stage1:
+            ps_z = stage1.enter_context(tc.psum_pool(name="ps_z", bufs=4))
+            ps_rows = stage1.enter_context(tc.psum_pool(name="ps_rows", bufs=4))
+            w_pool = stage1.enter_context(tc.tile_pool(name="w_pool", bufs=4))
+            relu_pool = stage1.enter_context(tc.tile_pool(name="relu_pool", bufs=8))
+            time_pool = stage1.enter_context(tc.tile_pool(name="time_pool", bufs=2))
+            once = stage1.enter_context(tc.tile_pool(name="once", bufs=1))
+
+            xT_ps = ps_z.tile([P, TOKENS], BF16, tag="z")
+            for b in range(BATCH):
+                nc.tensor.transpose(
+                    out=xT_ps[:, b * SEQ : (b + 1) * SEQ], in_=x_rows[:, b, :], identity=ident_bf[:]
+                )
+            nc.vector.tensor_copy(out=xT[:], in_=xT_ps[:])
+            bias_ps = ps_z.tile([P, P], BF16, tag="z")
+            nc.tensor.transpose(out=bias_ps[:], in_=bias_rows[:], identity=ident_bf[:])
+            nc.vector.tensor_copy(out=bias_col[:], in_=bias_ps[:, 0:N_TILES])
+
+            def timing_rows(g):
+                j = g % SINE_GROUPS
+                is_cos = g >= SINE_GROUPS
+                shift = half_pi if is_cos else zero_col
+                rows = time_pool.tile([P, K_PASS], F32, tag="timing")
+                if (SEQ - 1) * inv_timescale(K_PASS * j) + math.pi / 2 <= math.pi:
+                    nc.scalar.activation(
+                        out=rows[:], in_=w_base[:], func=ACT.Sin, bias=shift[:], scale=pos_w[:, j : j + 1]
+                    )
+                else:
+                    angle = once.tile([P, K_PASS], F32, tag="angle")
+                    nc.vector.tensor_scalar_mul(out=angle[:], in0=w_base[:], scalar1=pos_w[:, j : j + 1])
+                    turns = once.tile([P, K_PASS], I32, tag="turns")
+                    nc.vector.tensor_scalar(
+                        out=turns[:], in0=angle[:], scalar1=0.5 / math.pi, scalar2=0.25 if is_cos else 0.0,
+                        op0=ALU.mult, op1=ALU.add,
+                    )
+                    nc.vector.scalar_tensor_tensor(
+                        out=angle[:], in0=turns[:], scalar=-2.0 * math.pi, in1=angle[:], op0=ALU.mult, op1=ALU.add
+                    )
+                    nc.scalar.activation(out=rows[:], in_=angle[:], func=ACT.Sin, bias=shift[:], scale=1.0)
+                return rows
+
+            def embed_relu(g):
+                w_cols = w_pool.tile([P, K_PASS], BF16, tag="w_cols")
+                nc.gpsimd.dma_start(out=w_cols[:], in_=W_emb[:, g * K_PASS : (g + 1) * K_PASS])
+                tiles = []
+                for t in range(PACK):
+                    z = ps_z.tile([P, TOKENS], F32, tag="z")
+                    nc.tensor.matmul(out=z[:], lhsT=w_cols[:, t:K_PASS:PACK], rhs=xT[:], start=True, stop=True)
+                    r = relu_pool.tile([P, TOKENS], F32, tag="relu")
+                    c = g * PACK + t
+                    nc.scalar.activation(out=r[:], in_=z[:], func=ACT.Relu, bias=bias_emb[:, c : c + 1], scale=1.0)
+                    tiles.append(r)
+                return tiles
+
+            def add_timing(g, relu_tiles, timing):
+                for b in range(BATCH):
+                    rows = ps_rows.tile([P, K_PASS], F32, tag="rows")
+                    for t in range(PACK):
+                        nc.tensor.transpose(
+                            out=rows[:, t * P : (t + 1) * P],
+                            in_=relu_tiles[t][:, b * SEQ : (b + 1) * SEQ],
+                            identity=ident_f32[:],
+                        )
+                    nc.vector.scalar_tensor_tensor(
+                        out=e_rows[g][:, b, :], in0=rows[:], scalar=0.0, in1=timing[:],
+                        op0=ALU.add, op1=ALU.add, accum_out=sum_e[:, b, g : g + 1],
+                    )
+
+            def sum_squares(g):
+                for b in range(BATCH):
+                    if g % 2 == 0:
+                        junk_s = once.tile([P, K_PASS], BF16, tag="junk_s")
+                        nc.scalar.activation(
+                            out=junk_s[:], in_=e_rows[g][:, b, :], func=ACT.Square,
+                            accum_out=sq_scalar[:, b, g // 2 : g // 2 + 1],
+                        )
+                    else:
+                        junk_v = once.tile([P, K_PASS], F32, tag="junk_v")
+                        nc.vector.scalar_tensor_tensor(
+                            out=junk_v[:], in0=e_rows[g][:, b, :], scalar=1.0, in1=e_rows[g][:, b, :],
+                            op0=ALU.mult, op1=ALU.mult, accum_out=sq_vector[:, b, g // 2 : g // 2 + 1],
+                        )
+
+            relu_next = embed_relu(0)
+            timing_next = timing_rows(0)
+            for g in range(GROUPS):
+                relu_now, timing_now = relu_next, timing_next
+                if g + 1 < GROUPS:
+                    relu_next = embed_relu(g + 1)
+                    timing_next = timing_rows(g + 1)
+                add_timing(g, relu_now, timing_now)
+                sum_squares(g)
+
+        total = keep.tile([P, BATCH], F32)
+        nc.vector.tensor_reduce(out=total[:], in_=sum_e[:], axis=AXIS.X, op=ALU.add)
+        sq_a = keep.tile([P, BATCH], F32)
+        nc.vector.tensor_reduce(out=sq_a[:], in_=sq_scalar[:], axis=AXIS.X, op=ALU.add)
+        sq_b = keep.tile([P, BATCH], F32)
+        nc.vector.tensor_reduce(out=sq_b[:], in_=sq_vector[:], axis=AXIS.X, op=ALU.add)
+        mean = keep.tile([P, BATCH], F32)
+        nc.vector.tensor_scalar_mul(out=mean[:], in0=total[:], scalar1=1.0 / D)
+        mean_sq = keep.tile([P, BATCH], F32)
+        nc.vector.tensor_mul(out=mean_sq[:], in0=mean[:], in1=mean[:])
+        sq_sum = keep.tile([P, BATCH], F32)
+        nc.vector.tensor_add(out=sq_sum[:], in0=sq_a[:], in1=sq_b[:])
+        var = keep.tile([P, BATCH], F32)
+        nc.vector.scalar_tensor_tensor(
+            out=var[:], in0=sq_sum[:], scalar=1.0 / D, in1=mean_sq[:], op0=ALU.mult, op1=ALU.subtract
+        )
+        std = keep.tile([P, BATCH], F32)
+        nc.scalar.activation(out=std[:], in_=var[:], func=ACT.Sqrt, bias=eps_col[:], scale=1.0)
+        rstd = keep.tile([P, BATCH], F32)
+        nc.vector.reciprocal(out=rstd[:], in_=std[:])
+        neg_mean_rstd = keep.tile([P, BATCH], F32)
+        nc.vector.scalar_tensor_tensor(
+            out=neg_mean_rstd[:], in0=mean[:], scalar=-1.0, in1=rstd[:], op0=ALU.mult, op1=ALU.mult
+        )
+
+        with ExitStack() as stage2:
+            ps_acc = stage2.enter_context(tc.psum_pool(name="ps_acc", bufs=1))
+            ps_turn = stage2.enter_context(tc.psum_pool(name="ps_turn", bufs=2))
+            acc = [ps_acc.tile([P, TOKENS], F32, name="acc%d" % j) for j in range(N_TILES)]
+
+            def normalise(g):
+                for b in range(BATCH):
+                    nc.vector.tensor_scalar(
+                        out=e_rows[g][:, b, :], in0=e_rows[g][:, b, :],
+                        scalar1=rstd[:, b : b + 1], scalar2=neg_mean_rstd[:, b : b + 1],
+                        op0=ALU.mult, op1=ALU.add,
+                    )
+
+            def gain_and_beta(g, pool):
+                h_T = pool.tile([P, PACK, TOKENS], BF16, tag="h_T")
+                for t in range(PACK):
+                    turned = ps_turn.tile([P, TOKENS], F32, tag="turned")
+                    for b in range(BATCH):
+                        nc.tensor.transpose(
+                            out=turned[:, b * SEQ : (b + 1) * SEQ],
+                            in_=e_rows[g][:, b, t * P : (t + 1) * P],
+                            identity=ident_f32[:],
+                        )
+                    c = g * PACK + t
+                    nc.scalar.activation(
+                        out=h_T[:, t, :], in_=turned[:], func=ACT.Identity,
+                        bias=beta[:, c : c + 1], scale=gain[:, c : c + 1],
+                    )
+                return h_T
+
+            def regroup(h_T, pool):
+                grouped = pool.tile([P, TOKENS, PACK], BF16, tag="grouped", align_bytes=64)
+                nc.vector.tensor_copy(out=grouped[:], in_=h_T[:].rearrange("p t w -> p w t"))
+                return grouped
+
+            def quantise(grouped, pool):
+                codes = pool.tile([P, TOKENS], U32, tag="codes", align_bytes=64)
+                plane = pool.tile([P, TOKENS], U8, tag="plane", align_bytes=64)
+                nc.vector.quantize_mx(
+                    out=codes[:].bitcast(FP8X4), scales=plane[:], in_=grouped[:].rearrange("p w t -> p (w t)")
+                )
+                return codes, plane
+
+            def project(g, codes, plane):
+                for j in range(N_TILES):
+                    cols = slice(j * P, (j + 1) * P)
+                    nc.tensor.matmul_mx(
+                        out=acc[j][:],
+                        lhsT=w_words[:, g, cols].bitcast(FP8X4),
+                        lhsT_scale=w_planes[:, g, cols],
+                        rhs=codes[:].bitcast(FP8X4),
+                        rhs_scale=plane[:],
+                        start=(g == 0),
+                        stop=(g == GROUPS - 1),
+                    )
+
+            with tc.tile_pool(name="h_pool", bufs=2) as h_pool:
+                normalise(0)
+                ready = None
+                for g in range(GROUPS):
+                    if g + 1 < GROUPS:
+                        normalise(g + 1)
+                    h_T = gain_and_beta(g, h_pool)
+                    if ready is not None:
+                        project(g - 1, ready[0], ready[1])
+                    grouped = regroup(h_T, h_pool)
+                    ready = quantise(grouped, h_pool)
+                project(GROUPS - 1, ready[0], ready[1])
+
+            with tc.tile_pool(name="out_pool", bufs=2) as out_pool:
+                out_T = []
+                for j in range(N_TILES):
+                    o_T = out_pool.tile([P, TOKENS], F32, name="o_T%d" % j, bufs=1)
+                    if j % 2 == 0:
+                        nc.scalar.activation(
+                            out=o_T[:], in_=acc[j][:], func=ACT.Identity, bias=bias_col[:, j : j + 1], scale=1.0
+                        )
+                    else:
+                        nc.vector.tensor_scalar_add(out=o_T[:], in0=acc[j][:], scalar1=bias_col[:, j : j + 1])
+                    out_T.append(o_T)
+                for o in range(3):
+                    for pair in range(BATCH // 2):
+                        rows_ps = ps_turn.tile([P, 2, N_OUT], F32, tag="turned")
+                        for i in range(2):
+                            b = 2 * pair + i
+                            for half in range(2):
+                                nc.tensor.transpose(
+                                    out=rows_ps[:, i, half * P : (half + 1) * P],
+                                    in_=out_T[2 * o + half][:, b * SEQ : (b + 1) * SEQ],
+                                    identity=ident_f32[:],
+                                )
+                        rows = out_pool.tile([P, 2, N_OUT], F32, tag="rows")
+                        if pair == 0:
+                            nc.scalar.copy(out=rows[:], in_=rows_ps[:])
+                        else:
+                            nc.vector.tensor_copy(out=rows[:], in_=rows_ps[:])
+                        nc.sync.dma_start(
+                            out=outs[o][2 * pair : 2 * pair + 2].rearrange("b s n -> s b n"), in_=rows[:]
+                        )

@@ -28,6 +28,7 @@ N_ALL = 3 * N_OUT
 N_TILES = N_ALL // P
 EPS = 1e-3
 MAX_TIMESCALE = 10000.0
+W_AHEAD = 4
 
 FLOPS = 2 * TOKENS * P * D + 2 * TOKENS * D * N_ALL
 
@@ -46,53 +47,23 @@ def tile_ffnn_encoder_pa_k_kernel(
     outs = (out_0, out_1, out_2)
 
     with ExitStack() as ctx:
+        ctx.enter_context(tc.manual_schedule())
         keep = ctx.enter_context(tc.tile_pool(name="keep", bufs=1))
 
         x_rows = keep.tile([P, BATCH, P], BF16)
         nc.sync.dma_start(out=x_rows[:], in_=x.rearrange("b s f -> s b f"))
         vec_bf = keep.tile([P, 3, GROUPS, PACK], BF16)
         for i, vec in enumerate((b_emb, g0, beta0)):
-            nc.sync.dma_start(
+            nc.scalar.dma_start(
                 out=vec_bf[:, i], in_=vec.rearrange("(g m t) -> m g t", g=GROUPS, m=P, t=PACK)
             )
-        vec_f32 = keep.tile([P, 3, GROUPS * PACK], F32)
-        nc.vector.tensor_copy(out=vec_f32[:], in_=vec_bf[:].rearrange("p v g t -> p v (g t)"))
-        bias_emb, gain, beta = vec_f32[:, 0], vec_f32[:, 1], vec_f32[:, 2]
 
-        w_words = keep.tile([P, GROUPS, N_ALL], U32, align_bytes=64)
-        w_planes = keep.tile([P, GROUPS, N_ALL], U8, align_bytes=64)
-        nc.vector.memset(w_planes[:].rearrange("p g n -> p (g n)").bitcast(I32), 0)
-        bias_rows = keep.tile([P, P], BF16)
-        nc.vector.memset(bias_rows[:], 0.0)
-        for o, (words, scales, bias) in enumerate(weights):
-            cols = slice(o * N_OUT, (o + 1) * N_OUT)
-            nc.sync.dma_start(out=bias_rows[2 * o : 2 * o + 2, :], in_=bias.rearrange("(h n) -> h n", h=2))
-            for quad in range(4):
-                nc.sync.dma_start(
-                    out=w_planes[32 * quad : 32 * quad + 4, :, cols].bitcast(I32),
-                    in_=scales.rearrange("g q n -> q g n")[4 * quad : 4 * quad + 4].bitcast(I32),
-                )
-        for o, (words, scales, bias) in enumerate(weights):
-            cols = slice(o * N_OUT, (o + 1) * N_OUT)
-            nc.sync.dma_start(
-                out=w_words[:, :, cols].bitcast(I32),
-                in_=words.rearrange("g p n t -> p g (n t)").bitcast(I32),
-            )
-
-        ident_f32 = keep.tile([P, P], F32)
-        make_identity(nc, ident_f32[:])
         ident_bf = keep.tile([P, P], BF16)
         make_identity(nc, ident_bf[:])
         pos_i = keep.tile([P, 1], I32)
         nc.gpsimd.iota(pos_i[:], pattern=[[0, 1]], base=0, channel_multiplier=1)
-        pos_f = keep.tile([P, 1], F32)
-        nc.vector.tensor_copy(out=pos_f[:], in_=pos_i[:])
-        zero_col = keep.tile([P, 1], F32)
-        nc.vector.memset(zero_col[:], 0.0)
-        half_pi = keep.tile([P, 1], F32)
-        nc.vector.tensor_scalar_add(out=half_pi[:], in0=zero_col[:], scalar1=math.pi / 2)
-        eps_col = keep.tile([P, 1], F32)
-        nc.vector.tensor_scalar_add(out=eps_col[:], in0=zero_col[:], scalar1=EPS)
+        ident_f32 = keep.tile([P, P], F32)
+        make_identity(nc, ident_f32[:])
 
         w_base = keep.tile([P, K_PASS], F32)
         nc.vector.memset(w_base[:, 0:1], 1.0)
@@ -106,124 +77,161 @@ def tile_ffnn_encoder_pa_k_kernel(
             nc.vector.tensor_scalar_mul(
                 out=w_base[:, n : 2 * n], in0=w_base[:, 0:n], scalar1=inv_timescale(1 << bit)
             )
+        pos_f = keep.tile([P, 1], F32)
+        nc.vector.tensor_copy(out=pos_f[:], in_=pos_i[:])
         pos_w = keep.tile([P, SINE_GROUPS], F32)
         for j in range(SINE_GROUPS):
             nc.vector.tensor_scalar_mul(
                 out=pos_w[:, j : j + 1], in0=pos_f[:], scalar1=inv_timescale(K_PASS * j)
             )
+        zero_col = keep.tile([P, 1], F32)
+        nc.vector.memset(zero_col[:], 0.0)
+        half_pi = keep.tile([P, 1], F32)
+        nc.vector.tensor_scalar_add(out=half_pi[:], in0=zero_col[:], scalar1=math.pi / 2)
+        eps_col = keep.tile([P, 1], F32)
+        nc.vector.tensor_scalar_add(out=eps_col[:], in0=zero_col[:], scalar1=EPS)
 
         sum_e = keep.tile([P, BATCH, GROUPS], F32)
-        sq_scalar = keep.tile([P, BATCH, GROUPS // 2], F32)
-        sq_vector = keep.tile([P, BATCH, GROUPS // 2], F32)
+        sq_scalar = keep.tile([P, BATCH // 2, GROUPS], F32)
+        sq_vector = keep.tile([P, BATCH // 2, GROUPS], F32)
         e_rows = [keep.tile([P, BATCH, K_PASS], F32, name="e_rows%d" % g) for g in range(GROUPS)]
         xT = keep.tile([P, TOKENS], BF16)
+        w_words = keep.tile([P, GROUPS, N_ALL], U32, align_bytes=64)
+        w_planes = keep.tile([P, GROUPS, N_ALL], U8, align_bytes=64)
+        bias_rows = keep.tile([P, P], BF16)
         bias_col = keep.tile([P, N_TILES], F32)
+        vec_f32 = keep.tile([P, 3, GROUPS * PACK], F32)
+        bias_emb, gain, beta = vec_f32[:, 0], vec_f32[:, 1], vec_f32[:, 2]
 
         with ExitStack() as stage1:
-            ps_z = stage1.enter_context(tc.psum_pool(name="ps_z", bufs=4))
-            ps_rows = stage1.enter_context(tc.psum_pool(name="ps_rows", bufs=4))
-            w_pool = stage1.enter_context(tc.tile_pool(name="w_pool", bufs=4))
-            relu_pool = stage1.enter_context(tc.tile_pool(name="relu_pool", bufs=8))
-            time_pool = stage1.enter_context(tc.tile_pool(name="time_pool", bufs=2))
+            ps_z = stage1.enter_context(tc.psum_pool(name="ps_z", bufs=PACK))
+            ps_rows = stage1.enter_context(tc.psum_pool(name="ps_rows", bufs=BATCH))
+            w_pool = stage1.enter_context(tc.tile_pool(name="w_pool", bufs=W_AHEAD))
+            relu_pool = stage1.enter_context(tc.tile_pool(name="relu_pool", bufs=2 * PACK))
+            time_pool = stage1.enter_context(tc.tile_pool(name="time_pool", bufs=3))
+            angle_pool = stage1.enter_context(tc.tile_pool(name="angle_pool", bufs=2))
             once = stage1.enter_context(tc.tile_pool(name="once", bufs=1))
 
+            def load_w_emb(g):
+                w_cols = w_pool.tile([P, K_PASS], BF16, tag="w_cols")
+                nc.sync.dma_start(out=w_cols[:], in_=W_emb[:, g * K_PASS : (g + 1) * K_PASS])
+                return w_cols
+
+            def timing_angles(g):
+                j = g % SINE_GROUPS
+                if (SEQ - 1) * inv_timescale(K_PASS * j) + math.pi / 2 <= math.pi:
+                    return w_base, pos_w[:, j : j + 1]
+                angle = angle_pool.tile([P, K_PASS], F32, tag="angle")
+                nc.gpsimd.tensor_scalar(
+                    out=angle[:], in0=w_base[:], scalar1=pos_w[:, j : j + 1], scalar2=0.0,
+                    op0=ALU.mult, op1=ALU.add,
+                )
+                turns = angle_pool.tile([P, K_PASS], I32, tag="turns")
+                nc.gpsimd.tensor_scalar(
+                    out=turns[:], in0=angle[:], scalar1=0.5 / math.pi,
+                    scalar2=0.25 if g >= SINE_GROUPS else 0.0, op0=ALU.mult, op1=ALU.add,
+                )
+                nc.vector.scalar_tensor_tensor(
+                    out=angle[:], in0=turns[:], scalar=-2.0 * math.pi, in1=angle[:], op0=ALU.mult, op1=ALU.add
+                )
+                return angle, 1.0
+
+            def timing_sines(g, angles):
+                timing = time_pool.tile([P, K_PASS], F32, tag="timing")
+                shift = half_pi if g >= SINE_GROUPS else zero_col
+                nc.scalar.activation(out=timing[:], in_=angles[0][:], func=ACT.Sin, bias=shift[:], scale=angles[1])
+                return timing
+
+            def embed_relu(g, t, w_cols):
+                z = ps_z.tile([P, TOKENS], F32, tag="z")
+                nc.tensor.matmul(out=z[:], lhsT=w_cols[:, t:K_PASS:PACK], rhs=xT[:], start=True, stop=True)
+                r = relu_pool.tile([P, TOKENS], F32, tag="relu")
+                c = g * PACK + t
+                nc.scalar.activation(out=r[:], in_=z[:], func=ACT.Relu, bias=bias_emb[:, c : c + 1], scale=1.0)
+                return r
+
+            def add_timing(g, b, relu_tiles, timing):
+                turned = ps_rows.tile([P, K_PASS], F32, tag="turned")
+                for t in range(PACK):
+                    nc.tensor.transpose(
+                        out=turned[:, t * P : (t + 1) * P],
+                        in_=relu_tiles[t][:, b * SEQ : (b + 1) * SEQ],
+                        identity=ident_f32[:],
+                    )
+                nc.vector.scalar_tensor_tensor(
+                    out=e_rows[g][:, b, :], in0=turned[:], scalar=0.0, in1=timing[:],
+                    op0=ALU.add, op1=ALU.add, accum_out=sum_e[:, b, g : g + 1],
+                )
+
+            def sum_squares(g):
+                for b in range(BATCH // 2):
+                    junk_s = once.tile([P, K_PASS], BF16, tag="junk_s")
+                    nc.scalar.activation(
+                        out=junk_s[:], in_=e_rows[g][:, b, :], func=ACT.Square, accum_out=sq_scalar[:, b, g : g + 1]
+                    )
+                for b in range(BATCH // 2):
+                    junk_v = once.tile([P, K_PASS], F32, tag="junk_v")
+                    half = e_rows[g][:, BATCH // 2 + b, :]
+                    nc.vector.scalar_tensor_tensor(
+                        out=junk_v[:], in0=half, scalar=1.0, in1=half,
+                        op0=ALU.mult, op1=ALU.mult, accum_out=sq_vector[:, b, g : g + 1],
+                    )
+
+            w_tiles = [load_w_emb(g) for g in range(W_AHEAD)]
             xT_ps = ps_z.tile([P, TOKENS], BF16, tag="z")
             for b in range(BATCH):
                 nc.tensor.transpose(
                     out=xT_ps[:, b * SEQ : (b + 1) * SEQ], in_=x_rows[:, b, :], identity=ident_bf[:]
                 )
             nc.vector.tensor_copy(out=xT[:], in_=xT_ps[:])
-            bias_ps = ps_z.tile([P, P], BF16, tag="z")
-            nc.tensor.transpose(out=bias_ps[:], in_=bias_rows[:], identity=ident_bf[:])
-            nc.vector.tensor_copy(out=bias_col[:], in_=bias_ps[:, 0:N_TILES])
+            nc.vector.tensor_copy(out=vec_f32[:], in_=vec_bf[:].rearrange("p v g t -> p v (g t)"))
 
-            def timing_rows(g):
-                j = g % SINE_GROUPS
-                is_cos = g >= SINE_GROUPS
-                shift = half_pi if is_cos else zero_col
-                rows = time_pool.tile([P, K_PASS], F32, tag="timing")
-                if (SEQ - 1) * inv_timescale(K_PASS * j) + math.pi / 2 <= math.pi:
-                    nc.scalar.activation(
-                        out=rows[:], in_=w_base[:], func=ACT.Sin, bias=shift[:], scale=pos_w[:, j : j + 1]
-                    )
-                else:
-                    angle = once.tile([P, K_PASS], F32, tag="angle")
-                    nc.vector.tensor_scalar_mul(out=angle[:], in0=w_base[:], scalar1=pos_w[:, j : j + 1])
-                    turns = once.tile([P, K_PASS], I32, tag="turns")
-                    nc.vector.tensor_scalar(
-                        out=turns[:], in0=angle[:], scalar1=0.5 / math.pi, scalar2=0.25 if is_cos else 0.0,
-                        op0=ALU.mult, op1=ALU.add,
-                    )
-                    nc.vector.scalar_tensor_tensor(
-                        out=angle[:], in0=turns[:], scalar=-2.0 * math.pi, in1=angle[:], op0=ALU.mult, op1=ALU.add
-                    )
-                    nc.scalar.activation(out=rows[:], in_=angle[:], func=ACT.Sin, bias=shift[:], scale=1.0)
-                return rows
+            relu_next = [embed_relu(0, t, w_tiles[0]) for t in range(PACK)]
+            timings = [timing_sines(g, timing_angles(g)) for g in range(2)]
 
-            def embed_relu(g):
-                w_cols = w_pool.tile([P, K_PASS], BF16, tag="w_cols")
-                nc.gpsimd.dma_start(out=w_cols[:], in_=W_emb[:, g * K_PASS : (g + 1) * K_PASS])
-                tiles = []
-                for t in range(PACK):
-                    z = ps_z.tile([P, TOKENS], F32, tag="z")
-                    nc.tensor.matmul(out=z[:], lhsT=w_cols[:, t:K_PASS:PACK], rhs=xT[:], start=True, stop=True)
-                    r = relu_pool.tile([P, TOKENS], F32, tag="relu")
-                    c = g * PACK + t
-                    nc.scalar.activation(out=r[:], in_=z[:], func=ACT.Relu, bias=bias_emb[:, c : c + 1], scale=1.0)
-                    tiles.append(r)
-                return tiles
-
-            def add_timing(g, relu_tiles, timing):
-                for b in range(BATCH):
-                    rows = ps_rows.tile([P, K_PASS], F32, tag="rows")
-                    for t in range(PACK):
-                        nc.tensor.transpose(
-                            out=rows[:, t * P : (t + 1) * P],
-                            in_=relu_tiles[t][:, b * SEQ : (b + 1) * SEQ],
-                            identity=ident_f32[:],
-                        )
-                    nc.vector.scalar_tensor_tensor(
-                        out=e_rows[g][:, b, :], in0=rows[:], scalar=0.0, in1=timing[:],
-                        op0=ALU.add, op1=ALU.add, accum_out=sum_e[:, b, g : g + 1],
+            nc.vector.memset(w_planes[:].rearrange("p g n -> p (g n)").bitcast(I32), 0)
+            nc.vector.memset(bias_rows[:], 0.0)
+            for o, (words, scales, bias) in enumerate(weights):
+                cols = slice(o * N_OUT, (o + 1) * N_OUT)
+                nc.sync.dma_start(out=bias_rows[2 * o : 2 * o + 2, :], in_=bias.rearrange("(h n) -> h n", h=2))
+                for quad in range(4):
+                    nc.sync.dma_start(
+                        out=w_planes[32 * quad : 32 * quad + 4, :, cols].bitcast(I32),
+                        in_=scales.rearrange("g q n -> q g n")[4 * quad : 4 * quad + 4].bitcast(I32),
                     )
 
-            def sum_squares(g):
-                for b in range(BATCH):
-                    if g % 2 == 0:
-                        junk_s = once.tile([P, K_PASS], BF16, tag="junk_s")
-                        nc.scalar.activation(
-                            out=junk_s[:], in_=e_rows[g][:, b, :], func=ACT.Square,
-                            accum_out=sq_scalar[:, b, g // 2 : g // 2 + 1],
-                        )
-                    else:
-                        junk_v = once.tile([P, K_PASS], F32, tag="junk_v")
-                        nc.vector.scalar_tensor_tensor(
-                            out=junk_v[:], in0=e_rows[g][:, b, :], scalar=1.0, in1=e_rows[g][:, b, :],
-                            op0=ALU.mult, op1=ALU.mult, accum_out=sq_vector[:, b, g // 2 : g // 2 + 1],
-                        )
-
-            relu_next = embed_relu(0)
-            timing_next = timing_rows(0)
             for g in range(GROUPS):
-                relu_now, timing_now = relu_next, timing_next
-                if g + 1 < GROUPS:
-                    relu_next = embed_relu(g + 1)
-                    timing_next = timing_rows(g + 1)
-                add_timing(g, relu_now, timing_now)
+                relu_now, relu_next = relu_next, []
+                for i in range(PACK):
+                    if g + 1 < GROUPS:
+                        relu_next.append(embed_relu(g + 1, i, w_tiles[g + 1]))
+                    add_timing(g, i, relu_now, timings[g])
+                if g + W_AHEAD < GROUPS:
+                    w_tiles.append(load_w_emb(g + W_AHEAD))
+                if g < len(weights):
+                    nc.sync.dma_start(
+                        out=w_words[:, :, g * N_OUT : (g + 1) * N_OUT].bitcast(I32),
+                        in_=weights[g][0].rearrange("g p n t -> p g (n t)").bitcast(I32),
+                    )
+                if g + 2 < GROUPS:
+                    angles = timing_angles(g + 2)
                 sum_squares(g)
+                if g + 2 < GROUPS:
+                    timings.append(timing_sines(g + 2, angles))
+            warm = once.tile([P, 1], F32, tag="warm")
+            nc.scalar.activation(
+                out=warm[:], in_=timings[GROUPS - 1][:, 0:1], func=ACT.Sqrt, bias=eps_col[:], scale=0.0
+            )
 
         total = keep.tile([P, BATCH], F32)
         nc.vector.tensor_reduce(out=total[:], in_=sum_e[:], axis=AXIS.X, op=ALU.add)
-        sq_a = keep.tile([P, BATCH], F32)
-        nc.vector.tensor_reduce(out=sq_a[:], in_=sq_scalar[:], axis=AXIS.X, op=ALU.add)
-        sq_b = keep.tile([P, BATCH], F32)
-        nc.vector.tensor_reduce(out=sq_b[:], in_=sq_vector[:], axis=AXIS.X, op=ALU.add)
         mean = keep.tile([P, BATCH], F32)
         nc.vector.tensor_scalar_mul(out=mean[:], in0=total[:], scalar1=1.0 / D)
         mean_sq = keep.tile([P, BATCH], F32)
         nc.vector.tensor_mul(out=mean_sq[:], in0=mean[:], in1=mean[:])
         sq_sum = keep.tile([P, BATCH], F32)
-        nc.vector.tensor_add(out=sq_sum[:], in0=sq_a[:], in1=sq_b[:])
+        nc.vector.tensor_reduce(out=sq_sum[:, 0 : BATCH // 2], in_=sq_scalar[:], axis=AXIS.X, op=ALU.add)
+        nc.vector.tensor_reduce(out=sq_sum[:, BATCH // 2 : BATCH], in_=sq_vector[:], axis=AXIS.X, op=ALU.add)
         var = keep.tile([P, BATCH], F32)
         nc.vector.scalar_tensor_tensor(
             out=var[:], in0=sq_sum[:], scalar=1.0 / D, in1=mean_sq[:], op0=ALU.mult, op1=ALU.subtract
@@ -242,34 +250,34 @@ def tile_ffnn_encoder_pa_k_kernel(
             ps_turn = stage2.enter_context(tc.psum_pool(name="ps_turn", bufs=2))
             acc = [ps_acc.tile([P, TOKENS], F32, name="acc%d" % j) for j in range(N_TILES)]
 
-            def normalise(g):
-                for b in range(BATCH):
+            def normalise(g, batch_entries):
+                for b in batch_entries:
                     nc.vector.tensor_scalar(
                         out=e_rows[g][:, b, :], in0=e_rows[g][:, b, :],
                         scalar1=rstd[:, b : b + 1], scalar2=neg_mean_rstd[:, b : b + 1],
                         op0=ALU.mult, op1=ALU.add,
                     )
 
-            def gain_and_beta(g, pool):
-                h_T = pool.tile([P, PACK, TOKENS], BF16, tag="h_T")
-                for t in range(PACK):
-                    turned = ps_turn.tile([P, TOKENS], F32, tag="turned")
-                    for b in range(BATCH):
-                        nc.tensor.transpose(
-                            out=turned[:, b * SEQ : (b + 1) * SEQ],
-                            in_=e_rows[g][:, b, t * P : (t + 1) * P],
-                            identity=ident_f32[:],
-                        )
-                    c = g * PACK + t
-                    nc.scalar.activation(
-                        out=h_T[:, t, :], in_=turned[:], func=ACT.Identity,
-                        bias=beta[:, c : c + 1], scale=gain[:, c : c + 1],
+            def gain_and_beta(g, t, h_T):
+                turned = ps_turn.tile([P, TOKENS], F32, tag="turned")
+                for b in range(BATCH):
+                    nc.tensor.transpose(
+                        out=turned[:, b * SEQ : (b + 1) * SEQ],
+                        in_=e_rows[g][:, b, t * P : (t + 1) * P],
+                        identity=ident_f32[:],
                     )
-                return h_T
+                c = g * PACK + t
+                nc.scalar.activation(
+                    out=h_T[:, t, :], in_=turned[:], func=ACT.Identity,
+                    bias=beta[:, c : c + 1], scale=gain[:, c : c + 1],
+                )
 
             def regroup(h_T, pool):
                 grouped = pool.tile([P, TOKENS, PACK], BF16, tag="grouped", align_bytes=64)
-                nc.vector.tensor_copy(out=grouped[:], in_=h_T[:].rearrange("p t w -> p w t"))
+                nc.vector.tensor_copy(
+                    out=grouped[:].rearrange("p (c i) t -> p c t i", i=4),
+                    in_=h_T[:].rearrange("p t (c i) -> p c t i", i=4),
+                )
                 return grouped
 
             def quantise(grouped, pool):
@@ -280,31 +288,49 @@ def tile_ffnn_encoder_pa_k_kernel(
                 )
                 return codes, plane
 
-            def project(g, codes, plane):
-                for j in range(N_TILES):
+            def project(g, n_tiles, quantised):
+                for j in n_tiles:
                     cols = slice(j * P, (j + 1) * P)
                     nc.tensor.matmul_mx(
                         out=acc[j][:],
                         lhsT=w_words[:, g, cols].bitcast(FP8X4),
                         lhsT_scale=w_planes[:, g, cols],
-                        rhs=codes[:].bitcast(FP8X4),
-                        rhs_scale=plane[:],
+                        rhs=quantised[0][:].bitcast(FP8X4),
+                        rhs_scale=quantised[1][:],
                         start=(g == 0),
                         stop=(g == GROUPS - 1),
                     )
 
+            first_tiles = range(0, N_TILES // 2)
+            last_tiles = range(N_TILES // 2, N_TILES)
             with tc.tile_pool(name="h_pool", bufs=2) as h_pool:
-                normalise(0)
-                ready = None
-                for g in range(GROUPS):
+                normalise(0, range(BATCH))
+                bias_ps = ps_turn.tile([P, P], BF16, tag="turned")
+                nc.tensor.transpose(out=bias_ps[:], in_=bias_rows[:], identity=ident_bf[:])
+                nc.vector.tensor_copy(out=bias_col[:], in_=bias_ps[:, 0:N_TILES])
+                h_tiles = {}
+                quantised = {}
+                for g in range(GROUPS + 2):
+                    if g < GROUPS:
+                        h_T = h_pool.tile([P, PACK, TOKENS], BF16, tag="h_T")
+                        h_tiles[g] = h_T
+                        for t in range(0, PACK // 2):
+                            gain_and_beta(g, t, h_tiles[g])
+                    if 0 <= g - 2:
+                        project(g - 2, last_tiles, quantised[g - 2])
+                    if 0 <= g - 1 < GROUPS:
+                        grouped = regroup(h_tiles[g - 1], h_pool)
                     if g + 1 < GROUPS:
-                        normalise(g + 1)
-                    h_T = gain_and_beta(g, h_pool)
-                    if ready is not None:
-                        project(g - 1, ready[0], ready[1])
-                    grouped = regroup(h_T, h_pool)
-                    ready = quantise(grouped, h_pool)
-                project(GROUPS - 1, ready[0], ready[1])
+                        normalise(g + 1, range(0, BATCH // 2))
+                    if 0 <= g - 1 < GROUPS:
+                        quantised[g - 1] = quantise(grouped, h_pool)
+                    if g + 1 < GROUPS:
+                        normalise(g + 1, range(BATCH // 2, BATCH))
+                    if g < GROUPS:
+                        for t in range(PACK // 2, PACK):
+                            gain_and_beta(g, t, h_tiles[g])
+                    if 0 <= g - 1 < GROUPS:
+                        project(g - 1, first_tiles, quantised[g - 1])
 
             with tc.tile_pool(name="out_pool", bufs=2) as out_pool:
                 out_T = []

@@ -92,16 +92,21 @@ def tile_ffnn_encoder_pa_k_kernel(
         nc.vector.tensor_scalar_add(out=eps_col[:], in0=zero_col[:], scalar1=EPS)
 
         sum_e = keep.tile([P, BATCH, GROUPS], F32)
-        sq_scalar = keep.tile([P, BATCH // 2, GROUPS], F32)
-        sq_vector = keep.tile([P, BATCH // 2, GROUPS], F32)
-        e_rows = [keep.tile([P, BATCH, K_PASS], F32, name="e_rows%d" % g) for g in range(GROUPS)]
+        sq_scalar = keep.tile([P, BATCH // 2, GROUPS // 2], F32)
+        sq_vector = keep.tile([P, BATCH // 2, GROUPS // 2], F32)
+        e_pairs = [keep.tile([P, BATCH, 2 * K_PASS], F32, name="e_pair%d" % i) for i in range(GROUPS // 2)]
+
+        def e_rows(g, b):
+            return e_pairs[g // 2][:, b, (g % 2) * K_PASS : (g % 2 + 1) * K_PASS]
+
         xT = keep.tile([P, TOKENS], BF16)
         w_words = keep.tile([P, GROUPS, N_ALL], U32, align_bytes=64)
         w_planes = keep.tile([P, GROUPS, N_ALL], U8, align_bytes=64)
         bias_rows = keep.tile([P, P], BF16)
         bias_col = keep.tile([P, N_TILES], F32)
-        vec_f32 = keep.tile([P, 3, GROUPS * PACK], F32)
-        bias_emb, gain, beta = vec_f32[:, 0], vec_f32[:, 1], vec_f32[:, 2]
+        gain_beta = keep.tile([P, 2, GROUPS * PACK], F32)
+        bias_emb = vec_bf[:, 0].rearrange("p g t -> p (g t)")
+        gain, beta = gain_beta[:, 0], gain_beta[:, 1]
 
         with ExitStack() as stage1:
             ps_z = stage1.enter_context(tc.psum_pool(name="ps_z", bufs=PACK))
@@ -159,22 +164,22 @@ def tile_ffnn_encoder_pa_k_kernel(
                         identity=ident_f32[:],
                     )
                 nc.vector.scalar_tensor_tensor(
-                    out=e_rows[g][:, b, :], in0=turned[:], scalar=0.0, in1=timing[:],
+                    out=e_rows(g, b), in0=turned[:], scalar=0.0, in1=timing[:],
                     op0=ALU.add, op1=ALU.add, accum_out=sum_e[:, b, g : g + 1],
                 )
 
-            def sum_squares(g):
+            def sum_squares(i):
                 for b in range(BATCH // 2):
-                    junk_s = once.tile([P, K_PASS], BF16, tag="junk_s")
+                    junk_s = once.tile([P, 2 * K_PASS], BF16, tag="junk_s")
                     nc.scalar.activation(
-                        out=junk_s[:], in_=e_rows[g][:, b, :], func=ACT.Square, accum_out=sq_scalar[:, b, g : g + 1]
+                        out=junk_s[:], in_=e_pairs[i][:, b, :], func=ACT.Square, accum_out=sq_scalar[:, b, i : i + 1]
                     )
                 for b in range(BATCH // 2):
-                    junk_v = once.tile([P, K_PASS], F32, tag="junk_v")
-                    half = e_rows[g][:, BATCH // 2 + b, :]
+                    junk_v = once.tile([P, 2 * K_PASS], BF16, tag="junk_v")
+                    half = e_pairs[i][:, BATCH // 2 + b, :]
                     nc.vector.scalar_tensor_tensor(
                         out=junk_v[:], in0=half, scalar=1.0, in1=half,
-                        op0=ALU.mult, op1=ALU.mult, accum_out=sq_vector[:, b, g : g + 1],
+                        op0=ALU.mult, op1=ALU.mult, accum_out=sq_vector[:, b, i : i + 1],
                     )
 
             w_tiles = [load_w_emb(g) for g in range(W_AHEAD)]
@@ -184,10 +189,10 @@ def tile_ffnn_encoder_pa_k_kernel(
                     out=xT_ps[:, b * SEQ : (b + 1) * SEQ], in_=x_rows[:, b, :], identity=ident_bf[:]
                 )
             nc.vector.tensor_copy(out=xT[:], in_=xT_ps[:])
-            nc.vector.tensor_copy(out=vec_f32[:], in_=vec_bf[:].rearrange("p v g t -> p v (g t)"))
 
             relu_next = [embed_relu(0, t, w_tiles[0]) for t in range(PACK)]
             timings = [timing_sines(g, timing_angles(g)) for g in range(2)]
+            nc.gpsimd.tensor_copy(out=gain_beta[:], in_=vec_bf[:, 1:3].rearrange("p v g t -> p v (g t)"))
 
             nc.vector.memset(w_planes[:].rearrange("p g n -> p (g n)").bitcast(I32), 0)
             nc.vector.memset(bias_rows[:], 0.0)
@@ -215,7 +220,8 @@ def tile_ffnn_encoder_pa_k_kernel(
                     )
                 if g + 2 < GROUPS:
                     angles = timing_angles(g + 2)
-                sum_squares(g)
+                if g % 2 == 1:
+                    sum_squares(g // 2)
                 if g + 2 < GROUPS:
                     timings.append(timing_sines(g + 2, angles))
             warm = once.tile([P, 1], F32, tag="warm")
@@ -253,7 +259,7 @@ def tile_ffnn_encoder_pa_k_kernel(
             def normalise(g, batch_entries):
                 for b in batch_entries:
                     nc.vector.tensor_scalar(
-                        out=e_rows[g][:, b, :], in0=e_rows[g][:, b, :],
+                        out=e_rows(g, b), in0=e_rows(g, b),
                         scalar1=rstd[:, b : b + 1], scalar2=neg_mean_rstd[:, b : b + 1],
                         op0=ALU.mult, op1=ALU.add,
                     )
@@ -263,7 +269,7 @@ def tile_ffnn_encoder_pa_k_kernel(
                 for b in range(BATCH):
                     nc.tensor.transpose(
                         out=turned[:, b * SEQ : (b + 1) * SEQ],
-                        in_=e_rows[g][:, b, t * P : (t + 1) * P],
+                        in_=e_rows(g, b)[:, t * P : (t + 1) * P],
                         identity=ident_f32[:],
                     )
                 c = g * PACK + t

@@ -28,7 +28,7 @@ N_ALL = 3 * N_OUT
 N_TILES = N_ALL // P
 EPS = 1e-3
 MAX_TIMESCALE = 10000.0
-W_AHEAD = 4
+D_TILES = D // P
 
 FLOPS = 2 * TOKENS * P * D + 2 * TOKENS * D * N_ALL
 
@@ -52,8 +52,11 @@ def tile_ffnn_encoder_pa_k_kernel(
 
         x_rows = keep.tile([P, BATCH, P], BF16)
         nc.sync.dma_start(out=x_rows[:], in_=x.rearrange("b s f -> s b f"))
-        vec_bf = keep.tile([P, 3, GROUPS, PACK], BF16)
-        for i, vec in enumerate((b_emb, g0, beta0)):
+        b_rows = keep.tile([P, P], BF16)
+        nc.vector.memset(b_rows[:], 0.0)
+        nc.sync.dma_start(out=b_rows[0:D_TILES, :], in_=b_emb.rearrange("(c i) -> c i", i=P))
+        vec_bf = keep.tile([P, 2, GROUPS, PACK], BF16)
+        for i, vec in enumerate((g0, beta0)):
             nc.scalar.dma_start(
                 out=vec_bf[:, i], in_=vec.rearrange("(g m t) -> m g t", g=GROUPS, m=P, t=PACK)
             )
@@ -92,12 +95,11 @@ def tile_ffnn_encoder_pa_k_kernel(
         nc.vector.tensor_scalar_add(out=eps_col[:], in0=zero_col[:], scalar1=EPS)
 
         sum_e = keep.tile([P, BATCH, GROUPS], F32)
-        sq_scalar = keep.tile([P, BATCH // 2, GROUPS // 2], F32)
-        sq_vector = keep.tile([P, BATCH // 2, GROUPS // 2], F32)
-        e_pairs = [keep.tile([P, BATCH, 2 * K_PASS], F32, name="e_pair%d" % i) for i in range(GROUPS // 2)]
+        sum_sq = keep.tile([P, BATCH, GROUPS], F32)
+        e_tiles = [keep.tile([P, BATCH, K_PASS], F32, name="e_tile%d" % g) for g in range(GROUPS)]
 
         def e_rows(g, b):
-            return e_pairs[g // 2][:, b, (g % 2) * K_PASS : (g % 2 + 1) * K_PASS]
+            return e_tiles[g][:, b, :]
 
         xT = keep.tile([P, TOKENS], BF16)
         w_words = keep.tile([P, GROUPS, N_ALL], U32, align_bytes=64)
@@ -105,14 +107,12 @@ def tile_ffnn_encoder_pa_k_kernel(
         bias_rows = keep.tile([P, P], BF16)
         bias_col = keep.tile([P, N_TILES], F32)
         gain_beta = keep.tile([P, 2, GROUPS * PACK], F32)
-        bias_emb = vec_bf[:, 0].rearrange("p g t -> p (g t)")
+        bias_emb = keep.tile([P, D_TILES], F32)
         gain, beta = gain_beta[:, 0], gain_beta[:, 1]
 
         with ExitStack() as stage1:
-            ps_z = stage1.enter_context(tc.psum_pool(name="ps_z", bufs=PACK))
-            ps_rows = stage1.enter_context(tc.psum_pool(name="ps_rows", bufs=BATCH))
-            w_pool = stage1.enter_context(tc.tile_pool(name="w_pool", bufs=W_AHEAD))
-            relu_pool = stage1.enter_context(tc.tile_pool(name="relu_pool", bufs=2 * PACK))
+            ps_z = stage1.enter_context(tc.psum_pool(name="ps_z", bufs=8))
+            w_pool = stage1.enter_context(tc.tile_pool(name="w_pool", bufs=GROUPS))
             time_pool = stage1.enter_context(tc.tile_pool(name="time_pool", bufs=3))
             angle_pool = stage1.enter_context(tc.tile_pool(name="angle_pool", bufs=2))
             once = stage1.enter_context(tc.tile_pool(name="once", bufs=1))
@@ -147,52 +147,48 @@ def tile_ffnn_encoder_pa_k_kernel(
                 nc.scalar.activation(out=timing[:], in_=angles[0][:], func=ACT.Sin, bias=shift[:], scale=angles[1])
                 return timing
 
-            def embed_relu(g, t, w_cols):
-                z = ps_z.tile([P, TOKENS], F32, tag="z")
-                nc.tensor.matmul(out=z[:], lhsT=w_cols[:, t:K_PASS:PACK], rhs=xT[:], start=True, stop=True)
-                r = relu_pool.tile([P, TOKENS], F32, tag="relu")
-                c = g * PACK + t
-                nc.scalar.activation(out=r[:], in_=z[:], func=ACT.Relu, bias=bias_emb[:, c : c + 1], scale=1.0)
-                return r
-
-            def add_timing(g, b, relu_tiles, timing):
-                turned = ps_rows.tile([P, K_PASS], F32, tag="turned")
-                for t in range(PACK):
-                    nc.tensor.transpose(
-                        out=turned[:, t * P : (t + 1) * P],
-                        in_=relu_tiles[t][:, b * SEQ : (b + 1) * SEQ],
-                        identity=ident_f32[:],
+            def embed(g, b, w_cols, timing):
+                z = ps_z.tile([P, K_PASS], F32, tag="z")
+                nc.tensor.matmul(
+                    out=z[:], lhsT=xT[:, b * SEQ : (b + 1) * SEQ], rhs=w_cols[:], start=True, stop=False
+                )
+                for j in range(PACK):
+                    c = g * PACK + j
+                    nc.tensor.matmul(
+                        out=z[:, j * P : (j + 1) * P],
+                        lhsT=bias_emb[:, c : c + 1].to_broadcast([P, P]),
+                        rhs=ident_f32[:],
+                        is_transpose=True,
+                        start=False,
+                        stop=(j == PACK - 1),
                     )
                 nc.vector.scalar_tensor_tensor(
-                    out=e_rows(g, b), in0=turned[:], scalar=0.0, in1=timing[:],
-                    op0=ALU.add, op1=ALU.add, accum_out=sum_e[:, b, g : g + 1],
+                    out=e_rows(g, b).rearrange("p (t m) -> p t m", t=PACK),
+                    in0=z[:].rearrange("p (m t) -> p t m", t=PACK),
+                    scalar=0.0,
+                    in1=timing[:].rearrange("p (t m) -> p t m", t=PACK),
+                    op0=ALU.max, op1=ALU.add, accum_out=sum_e[:, b, g : g + 1],
                 )
 
-            def sum_squares(i):
-                for b in range(BATCH // 2):
-                    junk_s = once.tile([P, 2 * K_PASS], BF16, tag="junk_s")
-                    nc.scalar.activation(
-                        out=junk_s[:], in_=e_pairs[i][:, b, :], func=ACT.Square, accum_out=sq_scalar[:, b, i : i + 1]
-                    )
-                for b in range(BATCH // 2):
-                    junk_v = once.tile([P, 2 * K_PASS], BF16, tag="junk_v")
-                    half = e_pairs[i][:, BATCH // 2 + b, :]
-                    nc.vector.scalar_tensor_tensor(
-                        out=junk_v[:], in0=half, scalar=1.0, in1=half,
-                        op0=ALU.mult, op1=ALU.mult, accum_out=sq_vector[:, b, i : i + 1],
-                    )
+            def square(g, b):
+                junk = once.tile([P, K_PASS], BF16, tag="junk")
+                nc.scalar.activation(
+                    out=junk[:], in_=e_rows(g, b), func=ACT.Square, accum_out=sum_sq[:, b, g : g + 1]
+                )
 
-            w_tiles = [load_w_emb(g) for g in range(W_AHEAD)]
+            w_tiles = [load_w_emb(g) for g in range(GROUPS)]
             xT_ps = ps_z.tile([P, TOKENS], BF16, tag="z")
             for b in range(BATCH):
                 nc.tensor.transpose(
                     out=xT_ps[:, b * SEQ : (b + 1) * SEQ], in_=x_rows[:, b, :], identity=ident_bf[:]
                 )
             nc.vector.tensor_copy(out=xT[:], in_=xT_ps[:])
+            b_ps = ps_z.tile([P, P], BF16, tag="z")
+            nc.tensor.transpose(out=b_ps[:], in_=b_rows[:], identity=ident_bf[:])
+            nc.vector.tensor_copy(out=bias_emb[:], in_=b_ps[:, 0:D_TILES])
 
-            relu_next = [embed_relu(0, t, w_tiles[0]) for t in range(PACK)]
             timings = [timing_sines(g, timing_angles(g)) for g in range(2)]
-            nc.gpsimd.tensor_copy(out=gain_beta[:], in_=vec_bf[:, 1:3].rearrange("p v g t -> p v (g t)"))
+            nc.gpsimd.tensor_copy(out=gain_beta[:], in_=vec_bf[:].rearrange("p v g t -> p v (g t)"))
 
             nc.vector.memset(w_planes[:].rearrange("p g n -> p (g n)").bitcast(I32), 0)
             nc.vector.memset(bias_rows[:], 0.0)
@@ -204,26 +200,18 @@ def tile_ffnn_encoder_pa_k_kernel(
                         out=w_planes[32 * quad : 32 * quad + 4, :, cols].bitcast(I32),
                         in_=scales.rearrange("g q n -> q g n")[4 * quad : 4 * quad + 4].bitcast(I32),
                     )
+            for o, (words, scales, bias) in enumerate(weights):
+                nc.sync.dma_start(
+                    out=w_words[:, :, o * N_OUT : (o + 1) * N_OUT].bitcast(I32),
+                    in_=words.rearrange("g p n t -> p g (n t)").bitcast(I32),
+                )
 
             for g in range(GROUPS):
-                relu_now, relu_next = relu_next, []
-                for i in range(PACK):
-                    if g + 1 < GROUPS:
-                        relu_next.append(embed_relu(g + 1, i, w_tiles[g + 1]))
-                    add_timing(g, i, relu_now, timings[g])
-                if g + W_AHEAD < GROUPS:
-                    w_tiles.append(load_w_emb(g + W_AHEAD))
-                if g < len(weights):
-                    nc.sync.dma_start(
-                        out=w_words[:, :, g * N_OUT : (g + 1) * N_OUT].bitcast(I32),
-                        in_=weights[g][0].rearrange("g p n t -> p g (n t)").bitcast(I32),
-                    )
+                for b in range(BATCH):
+                    embed(g, b, w_tiles[g], timings[g])
+                    square(g, b)
                 if g + 2 < GROUPS:
-                    angles = timing_angles(g + 2)
-                if g % 2 == 1:
-                    sum_squares(g // 2)
-                if g + 2 < GROUPS:
-                    timings.append(timing_sines(g + 2, angles))
+                    timings.append(timing_sines(g + 2, timing_angles(g + 2)))
             warm = once.tile([P, 1], F32, tag="warm")
             nc.scalar.activation(
                 out=warm[:], in_=timings[GROUPS - 1][:, 0:1], func=ACT.Sqrt, bias=eps_col[:], scale=0.0
@@ -236,8 +224,7 @@ def tile_ffnn_encoder_pa_k_kernel(
         mean_sq = keep.tile([P, BATCH], F32)
         nc.vector.tensor_mul(out=mean_sq[:], in0=mean[:], in1=mean[:])
         sq_sum = keep.tile([P, BATCH], F32)
-        nc.vector.tensor_reduce(out=sq_sum[:, 0 : BATCH // 2], in_=sq_scalar[:], axis=AXIS.X, op=ALU.add)
-        nc.vector.tensor_reduce(out=sq_sum[:, BATCH // 2 : BATCH], in_=sq_vector[:], axis=AXIS.X, op=ALU.add)
+        nc.vector.tensor_reduce(out=sq_sum[:], in_=sum_sq[:], axis=AXIS.X, op=ALU.add)
         var = keep.tile([P, BATCH], F32)
         nc.vector.scalar_tensor_tensor(
             out=var[:], in0=sq_sum[:], scalar=1.0 / D, in1=mean_sq[:], op0=ALU.mult, op1=ALU.subtract

@@ -147,11 +147,14 @@ def tile_ffnn_encoder_pa_k_kernel(
                 nc.scalar.activation(out=timing[:], in_=angles[0][:], func=ACT.Sin, bias=shift[:], scale=angles[1])
                 return timing
 
-            def embed(g, b, w_cols, timing):
+            def embed(g, b, w_cols):
                 z = ps_z.tile([P, K_PASS], F32, tag="z")
                 nc.tensor.matmul(
                     out=z[:], lhsT=xT[:, b * SEQ : (b + 1) * SEQ], rhs=w_cols[:], start=True, stop=False
                 )
+                return z
+
+            def bias_relu_timing(g, b, z, timing):
                 for j in range(PACK):
                     c = g * PACK + j
                     nc.tensor.matmul(
@@ -207,8 +210,9 @@ def tile_ffnn_encoder_pa_k_kernel(
                 )
 
             for g in range(GROUPS):
+                banks = [embed(g, b, w_tiles[g]) for b in range(BATCH)]
                 for b in range(BATCH):
-                    embed(g, b, w_tiles[g], timings[g])
+                    bias_relu_timing(g, b, banks[b], timings[g])
                     square(g, b)
                 if g + 2 < GROUPS:
                     timings.append(timing_sines(g + 2, timing_angles(g + 2)))

@@ -300,11 +300,12 @@ def tile_ffnn_encoder_pa_k_kernel(
 
             first_tiles = range(0, N_TILES // 2)
             last_tiles = range(N_TILES // 2, N_TILES)
-            with tc.tile_pool(name="h_pool", bufs=2) as h_pool:
+            with tc.tile_pool(name="h_pool", bufs=2) as h_pool, tc.tile_pool(name="code_pool", bufs=3) as code_pool:
                 normalise(0, range(BATCH))
                 bias_ps = ps_turn.tile([P, P], BF16, tag="turned")
                 nc.tensor.transpose(out=bias_ps[:], in_=bias_rows[:], identity=ident_bf[:])
                 nc.vector.tensor_copy(out=bias_col[:], in_=bias_ps[:, 0:N_TILES])
+                normalise(1, range(BATCH))
                 h_tiles = {}
                 quantised = {}
                 for g in range(GROUPS + 2):
@@ -314,20 +315,20 @@ def tile_ffnn_encoder_pa_k_kernel(
                         for t in range(0, PACK // 2):
                             gain_and_beta(g, t, h_tiles[g])
                     if 0 <= g - 2:
-                        project(g - 2, last_tiles, quantised[g - 2])
+                        project(g - 2, first_tiles, quantised[g - 2])
+                    if g + 2 < GROUPS:
+                        normalise(g + 2, range(0, BATCH // 2))
                     if 0 <= g - 1 < GROUPS:
                         grouped = regroup(h_tiles[g - 1], h_pool)
-                    if g + 1 < GROUPS:
-                        normalise(g + 1, range(0, BATCH // 2))
+                    if g + 2 < GROUPS:
+                        normalise(g + 2, range(BATCH // 2, BATCH))
                     if 0 <= g - 1 < GROUPS:
-                        quantised[g - 1] = quantise(grouped, h_pool)
-                    if g + 1 < GROUPS:
-                        normalise(g + 1, range(BATCH // 2, BATCH))
+                        quantised[g - 1] = quantise(grouped, code_pool)
                     if g < GROUPS:
                         for t in range(PACK // 2, PACK):
                             gain_and_beta(g, t, h_tiles[g])
-                    if 0 <= g - 1 < GROUPS:
-                        project(g - 1, first_tiles, quantised[g - 1])
+                    if 0 <= g - 2:
+                        project(g - 2, last_tiles, quantised[g - 2])
 
             with tc.tile_pool(name="out_pool", bufs=2) as out_pool:
                 out_T = []

@@ -271,10 +271,7 @@ def tile_ffnn_encoder_pa_k_kernel(
 
             def regroup(h_T, pool):
                 grouped = pool.tile([P, TOKENS, PACK], BF16, tag="grouped", align_bytes=64)
-                nc.vector.tensor_copy(
-                    out=grouped[:].rearrange("p (c i) t -> p c t i", i=4),
-                    in_=h_T[:].rearrange("p t (c i) -> p c t i", i=4),
-                )
+                nc.vector.tensor_copy(out=grouped[:], in_=h_T[:].rearrange("p t w -> p w t"))
                 return grouped
 
             def quantise(grouped, pool):

@@ -25,7 +25,12 @@ GROUPS = D // K_PASS
 SINE_GROUPS = GROUPS // 2
 N_OUT = 256
 N_ALL = 3 * N_OUT
-N_TILES = N_ALL // P
+N_QK = 2 * N_OUT
+SWEEPS = 2
+HALF = BATCH // SWEEPS
+HALF_TOKENS = HALF * SEQ
+PAIRS = GROUPS // 2
+ROUNDS = SWEEPS * PAIRS
 EPS = 1e-3
 MAX_TIMESCALE = 10000.0
 D_TILES = D // P
@@ -104,8 +109,7 @@ def tile_ffnn_encoder_pa_k_kernel(
         xT = keep.tile([P, TOKENS], BF16)
         w_words = keep.tile([P, GROUPS, N_ALL], U32, align_bytes=64)
         w_planes = keep.tile([P, GROUPS, N_ALL], U8, align_bytes=64)
-        bias_rows = keep.tile([P, P], BF16)
-        bias_col = keep.tile([P, N_TILES], F32)
+        bias_all = keep.tile([P, N_ALL], BF16)
         gain_beta = keep.tile([P, 2, GROUPS * PACK], F32)
         bias_emb = keep.tile([P, D_TILES], F32)
         gain, beta = gain_beta[:, 0], gain_beta[:, 1]
@@ -194,10 +198,8 @@ def tile_ffnn_encoder_pa_k_kernel(
             nc.gpsimd.tensor_copy(out=gain_beta[:], in_=vec_bf[:].rearrange("p v g t -> p v (g t)"))
 
             nc.vector.memset(w_planes[:].rearrange("p g n -> p (g n)").bitcast(I32), 0)
-            nc.vector.memset(bias_rows[:], 0.0)
             for o, (words, scales, bias) in enumerate(weights):
                 cols = slice(o * N_OUT, (o + 1) * N_OUT)
-                nc.sync.dma_start(out=bias_rows[2 * o : 2 * o + 2, :], in_=bias.rearrange("(h n) -> h n", h=2))
                 for quad in range(4):
                     nc.sync.dma_start(
                         out=w_planes[32 * quad : 32 * quad + 4, :, cols].bitcast(I32),
@@ -208,6 +210,8 @@ def tile_ffnn_encoder_pa_k_kernel(
                     out=w_words[:, :, o * N_OUT : (o + 1) * N_OUT].bitcast(I32),
                     in_=words.rearrange("g p n t -> p g (n t)").bitcast(I32),
                 )
+            for o, (words, scales, bias) in enumerate(weights):
+                nc.sync.dma_start(out=bias_all[:, o * N_OUT : (o + 1) * N_OUT], in_=bias.partition_broadcast(P))
 
             for g in range(GROUPS):
                 banks = [embed(g, b, w_tiles[g]) for b in range(BATCH)]
@@ -244,116 +248,115 @@ def tile_ffnn_encoder_pa_k_kernel(
 
         with ExitStack() as stage2:
             ps_acc = stage2.enter_context(tc.psum_pool(name="ps_acc", bufs=1))
-            ps_turn = stage2.enter_context(tc.psum_pool(name="ps_turn", bufs=2))
-            acc = [ps_acc.tile([P, TOKENS], F32, name="acc%d" % j) for j in range(N_TILES)]
+            ps_turn = stage2.enter_context(tc.psum_pool(name="ps_turn", bufs=4))
+            h_pool = stage2.enter_context(tc.tile_pool(name="h_pool", bufs=2))
+            code_pool = stage2.enter_context(tc.tile_pool(name="code_pool", bufs=3))
+            out_pool = stage2.enter_context(tc.tile_pool(name="out_pool", bufs=2))
 
-            def normalise(g, batch_entries):
-                for b in batch_entries:
-                    nc.vector.tensor_scalar(
-                        out=e_rows(g, b), in0=e_rows(g, b),
-                        scalar1=rstd[:, b : b + 1], scalar2=neg_mean_rstd[:, b : b + 1],
-                        op0=ALU.mult, op1=ALU.add,
-                    )
+            def groups_of(r):
+                return (2 * (r % PAIRS), 2 * (r % PAIRS) + 1)
 
-            def gain_and_beta(g, t, h_T):
-                turned = ps_turn.tile([P, TOKENS], F32, tag="turned")
-                for b in range(BATCH):
-                    nc.tensor.transpose(
-                        out=turned[:, b * SEQ : (b + 1) * SEQ],
-                        in_=e_rows(g, b)[:, t * P : (t + 1) * P],
-                        identity=ident_f32[:],
-                    )
-                c = g * PACK + t
-                nc.scalar.activation(
-                    out=h_T[:, t, :], in_=turned[:], func=ACT.Identity,
-                    bias=beta[:, c : c + 1], scale=gain[:, c : c + 1],
+            def entries_of(r):
+                return tuple(range(HALF * (r // PAIRS), HALF * (r // PAIRS) + HALF))
+
+            def normalise(g, b):
+                nc.vector.tensor_scalar(
+                    out=e_rows(g, b), in0=e_rows(g, b),
+                    scalar1=rstd[:, b : b + 1], scalar2=neg_mean_rstd[:, b : b + 1],
+                    op0=ALU.mult, op1=ALU.add,
                 )
 
-            def regroup(h_T, pool):
-                grouped = pool.tile([P, TOKENS, PACK], BF16, tag="grouped", align_bytes=64)
-                nc.vector.tensor_copy(out=grouped[:], in_=h_T[:].rearrange("p t w -> p w t"))
+            def gain_and_beta(g, entries, t_pair, h_slot):
+                turned = ps_turn.tile([P, 2, HALF_TOKENS], F32, tag="turned")
+                for u in range(2):
+                    t = 2 * t_pair + u
+                    for i, b in enumerate(entries):
+                        nc.tensor.transpose(
+                            out=turned[:, u, i * SEQ : (i + 1) * SEQ],
+                            in_=e_rows(g, b)[:, t * P : (t + 1) * P],
+                            identity=ident_f32[:],
+                        )
+                for u in range(2):
+                    t = 2 * t_pair + u
+                    c = g * PACK + t
+                    nc.scalar.activation(
+                        out=h_slot[:, t, :], in_=turned[:, u, :], func=ACT.Identity,
+                        bias=beta[:, c : c + 1], scale=gain[:, c : c + 1],
+                    )
+
+            def regroup(h_T):
+                grouped = h_pool.tile([P, 2, HALF_TOKENS, PACK], BF16, tag="grouped", align_bytes=64)
+                nc.vector.tensor_copy(out=grouped[:], in_=h_T[:].rearrange("p k t w -> p k w t"))
                 return grouped
 
-            def quantise(grouped, pool):
-                codes = pool.tile([P, TOKENS], U32, tag="codes", align_bytes=64)
-                plane = pool.tile([P, TOKENS], U8, tag="plane", align_bytes=64)
+            def quantise(grouped):
+                codes = code_pool.tile([P, 2, HALF_TOKENS], U32, tag="codes", align_bytes=64)
+                plane = code_pool.tile([P, 2, HALF_TOKENS], U8, tag="plane", align_bytes=64)
                 nc.vector.quantize_mx(
-                    out=codes[:].bitcast(FP8X4), scales=plane[:], in_=grouped[:].rearrange("p w t -> p (w t)")
+                    out=codes[:].rearrange("p k w -> p (k w)").bitcast(FP8X4),
+                    scales=plane[:].rearrange("p k w -> p (k w)"),
+                    in_=grouped[:].rearrange("p k w t -> p (k w t)"),
                 )
                 return codes, plane
 
-            def project(g, n_tiles, quantised):
-                for j in n_tiles:
-                    cols = slice(j * P, (j + 1) * P)
-                    nc.tensor.matmul_mx(
-                        out=acc[j][:],
-                        lhsT=w_words[:, g, cols].bitcast(FP8X4),
-                        lhsT_scale=w_planes[:, g, cols],
-                        rhs=quantised[0][:].bitcast(FP8X4),
-                        rhs_scale=quantised[1][:],
-                        start=(g == 0),
-                        stop=(g == GROUPS - 1),
+            def project(g, k, quantised, acc):
+                for i in range(HALF):
+                    tokens = slice(i * SEQ, (i + 1) * SEQ)
+                    for bank, cols in ((acc[i][0][:], slice(0, N_QK)), (acc[i][1][:, 0:N_OUT], slice(N_QK, N_ALL))):
+                        nc.tensor.matmul_mx(
+                            out=bank,
+                            lhsT=quantised[0][:, k, tokens].bitcast(FP8X4),
+                            lhsT_scale=quantised[1][:, k, tokens],
+                            rhs=w_words[:, g, cols].bitcast(FP8X4),
+                            rhs_scale=w_planes[:, g, cols],
+                            start=(g == 0),
+                            stop=(g == GROUPS - 1),
+                        )
+
+            def store(entries, acc):
+                for i, b in enumerate(entries):
+                    rows_qk = out_pool.tile([P, N_QK], F32, tag="rows_qk")
+                    nc.vector.tensor_tensor(out=rows_qk[:], in0=acc[i][0][:], in1=bias_all[:, 0:N_QK], op=ALU.add)
+                    nc.sync.dma_start(out=outs[0][b], in_=rows_qk[:, 0:N_OUT])
+                    nc.sync.dma_start(out=outs[1][b], in_=rows_qk[:, N_OUT:N_QK])
+                    rows_v = out_pool.tile([P, N_OUT], F32, tag="rows_v")
+                    nc.vector.tensor_tensor(
+                        out=rows_v[:], in0=acc[i][1][:, 0:N_OUT], in1=bias_all[:, N_QK:N_ALL], op=ALU.add
                     )
+                    nc.sync.dma_start(out=outs[2][b], in_=rows_v[:])
 
-            first_tiles = range(0, N_TILES // 2)
-            last_tiles = range(N_TILES // 2, N_TILES)
-            with tc.tile_pool(name="h_pool", bufs=2) as h_pool, tc.tile_pool(name="code_pool", bufs=3) as code_pool:
-                normalise(0, range(BATCH))
-                bias_ps = ps_turn.tile([P, P], BF16, tag="turned")
-                nc.tensor.transpose(out=bias_ps[:], in_=bias_rows[:], identity=ident_bf[:])
-                nc.vector.tensor_copy(out=bias_col[:], in_=bias_ps[:, 0:N_TILES])
-                normalise(1, range(BATCH))
-                h_tiles = {}
-                quantised = {}
-                for g in range(GROUPS + 2):
-                    if g < GROUPS:
-                        h_T = h_pool.tile([P, PACK, TOKENS], BF16, tag="h_T")
-                        h_tiles[g] = h_T
-                        for t in range(0, PACK // 2):
-                            gain_and_beta(g, t, h_tiles[g])
-                    if 0 <= g - 2:
-                        project(g - 2, first_tiles, quantised[g - 2])
-                    if g + 2 < GROUPS:
-                        normalise(g + 2, range(0, BATCH // 2))
-                    if 0 <= g - 1 < GROUPS:
-                        grouped = regroup(h_tiles[g - 1], h_pool)
-                    if g + 2 < GROUPS:
-                        normalise(g + 2, range(BATCH // 2, BATCH))
-                    if 0 <= g - 1 < GROUPS:
-                        quantised[g - 1] = quantise(grouped, code_pool)
-                    if g < GROUPS:
-                        for t in range(PACK // 2, PACK):
-                            gain_and_beta(g, t, h_tiles[g])
-                    if 0 <= g - 2:
-                        project(g - 2, last_tiles, quantised[g - 2])
-
-            with tc.tile_pool(name="out_pool", bufs=2) as out_pool:
-                out_T = []
-                for j in range(N_TILES):
-                    o_T = out_pool.tile([P, TOKENS], F32, name="o_T%d" % j, bufs=1)
-                    if j % 2 == 0:
-                        nc.scalar.activation(
-                            out=o_T[:], in_=acc[j][:], func=ACT.Identity, bias=bias_col[:, j : j + 1], scale=1.0
-                        )
-                    else:
-                        nc.vector.tensor_scalar_add(out=o_T[:], in0=acc[j][:], scalar1=bias_col[:, j : j + 1])
-                    out_T.append(o_T)
-                for o in range(3):
-                    for pair in range(BATCH // 2):
-                        rows_ps = ps_turn.tile([P, 2, N_OUT], F32, tag="turned")
-                        for i in range(2):
-                            b = 2 * pair + i
-                            for half in range(2):
-                                nc.tensor.transpose(
-                                    out=rows_ps[:, i, half * P : (half + 1) * P],
-                                    in_=out_T[2 * o + half][:, b * SEQ : (b + 1) * SEQ],
-                                    identity=ident_f32[:],
+            for r in range(2):
+                for g in groups_of(r):
+                    for b in entries_of(r):
+                        normalise(g, b)
+            h_tiles = {}
+            quantised = {}
+            acc = None
+            for r in range(ROUNDS + 2):
+                ahead = [(g, b) for g in groups_of(r + 2) for b in entries_of(r + 2)] if r + 2 < ROUNDS else []
+                if r < ROUNDS:
+                    h_T = h_pool.tile([P, 2, PACK, HALF_TOKENS], BF16, tag="h_T")
+                    h_tiles[r] = h_T
+                for k in range(2):
+                    if r < ROUNDS:
+                        for t_pair in range(PACK // 2):
+                            gain_and_beta(groups_of(r)[k], entries_of(r), t_pair, h_tiles[r][:, k])
+                    if 0 <= r - 2:
+                        if k == 0 and (r - 2) % PAIRS == 0:
+                            acc = [
+                                (
+                                    ps_acc.tile([P, N_QK], F32, name="acc_qk%d" % i),
+                                    ps_acc.tile([P, N_QK], F32, name="acc_v%d" % i),
                                 )
-                        rows = out_pool.tile([P, 2, N_OUT], F32, tag="rows")
-                        if pair == 0:
-                            nc.scalar.copy(out=rows[:], in_=rows_ps[:])
+                                for i in range(HALF)
+                            ]
+                        project(groups_of(r - 2)[k], k, quantised[r - 2], acc)
+                    for g, b in ahead[2 * k : 2 * k + 2]:
+                        normalise(g, b)
+                    if 0 <= r - 1 < ROUNDS:
+                        if k == 0:
+                            grouped = regroup(h_tiles[r - 1])
                         else:
-                            nc.vector.tensor_copy(out=rows[:], in_=rows_ps[:])
-                        nc.sync.dma_start(
-                            out=outs[o][2 * pair : 2 * pair + 2].rearrange("b s n -> s b n"), in_=rows[:]
-                        )
+                            quantised[r - 1] = quantise(grouped)
+                if 0 <= r - 2 and (r - 2) % PAIRS == PAIRS - 1:
+                    store(entries_of(r - 2), acc)

@@ -34,12 +34,17 @@ ROUNDS = SWEEPS * PAIRS
 EPS = 1e-3
 MAX_TIMESCALE = 10000.0
 D_TILES = D // P
+T_AHEAD = 4
 
 FLOPS = 2 * TOKENS * P * D + 2 * TOKENS * D * N_ALL
 
 
 def inv_timescale(i):
     return MAX_TIMESCALE ** (-i / (D // 2 - 1.0))
+
+
+def in_sine_range(g):
+    return (SEQ - 1) * inv_timescale(K_PASS * (g % SINE_GROUPS)) + math.pi / 2 <= math.pi
 
 
 def tile_ffnn_encoder_pa_k_kernel(
@@ -61,10 +66,6 @@ def tile_ffnn_encoder_pa_k_kernel(
         nc.vector.memset(b_rows[:], 0.0)
         nc.sync.dma_start(out=b_rows[0:D_TILES, :], in_=b_emb.rearrange("(c i) -> c i", i=P))
         vec_bf = keep.tile([P, 2, GROUPS, PACK], BF16)
-        for i, vec in enumerate((g0, beta0)):
-            nc.scalar.dma_start(
-                out=vec_bf[:, i], in_=vec.rearrange("(g m t) -> m g t", g=GROUPS, m=P, t=PACK)
-            )
 
         ident_bf = keep.tile([P, P], BF16)
         make_identity(nc, ident_bf[:])
@@ -100,11 +101,11 @@ def tile_ffnn_encoder_pa_k_kernel(
         nc.vector.tensor_scalar_add(out=eps_col[:], in0=zero_col[:], scalar1=EPS)
 
         sum_e = keep.tile([P, BATCH, GROUPS], F32)
-        sum_sq = keep.tile([P, BATCH, GROUPS], F32)
-        e_tiles = [keep.tile([P, BATCH, K_PASS], F32, name="e_tile%d" % g) for g in range(GROUPS)]
+        sum_sq = keep.tile([P, BATCH, GROUPS // 2 + 1], F32)
+        e_pairs = [keep.tile([P, BATCH, 2 * K_PASS], F32, name="e_pair%d" % i) for i in range(GROUPS // 2)]
 
         def e_rows(g, b):
-            return e_tiles[g][:, b, :]
+            return e_pairs[g // 2][:, b, (g % 2) * K_PASS : (g % 2 + 1) * K_PASS]
 
         xT = keep.tile([P, TOKENS], BF16)
         w_words = keep.tile([P, GROUPS, N_ALL], U32, align_bytes=64)
@@ -117,7 +118,7 @@ def tile_ffnn_encoder_pa_k_kernel(
         with ExitStack() as stage1:
             ps_z = stage1.enter_context(tc.psum_pool(name="ps_z", bufs=8))
             w_pool = stage1.enter_context(tc.tile_pool(name="w_pool", bufs=GROUPS))
-            time_pool = stage1.enter_context(tc.tile_pool(name="time_pool", bufs=3))
+            time_pool = stage1.enter_context(tc.tile_pool(name="time_pool", bufs=T_AHEAD + 1))
             angle_pool = stage1.enter_context(tc.tile_pool(name="angle_pool", bufs=2))
             once = stage1.enter_context(tc.tile_pool(name="once", bufs=1))
 
@@ -128,7 +129,7 @@ def tile_ffnn_encoder_pa_k_kernel(
 
             def timing_angles(g):
                 j = g % SINE_GROUPS
-                if (SEQ - 1) * inv_timescale(K_PASS * j) + math.pi / 2 <= math.pi:
+                if in_sine_range(g):
                     return w_base, pos_w[:, j : j + 1]
                 angle = angle_pool.tile([P, K_PASS], F32, tag="angle")
                 nc.gpsimd.tensor_scalar(
@@ -177,13 +178,21 @@ def tile_ffnn_encoder_pa_k_kernel(
                     op0=ALU.max, op1=ALU.add, accum_out=sum_e[:, b, g : g + 1],
                 )
 
-            def square(g, b):
-                junk = once.tile([P, K_PASS], BF16, tag="junk")
+            def square(g, b, groups, column):
+                first = (g % 2 + 1 - groups) * K_PASS
+                junk = once.tile([P, 2 * K_PASS], BF16, tag="junk")
                 nc.scalar.activation(
-                    out=junk[:], in_=e_rows(g, b), func=ACT.Square, accum_out=sum_sq[:, b, g : g + 1]
+                    out=junk[:, 0 : groups * K_PASS], in_=e_pairs[g // 2][:, b, first : first + groups * K_PASS],
+                    func=ACT.Square, accum_out=sum_sq[:, b, column : column + 1],
                 )
 
-            w_tiles = [load_w_emb(g) for g in range(GROUPS)]
+            order = sorted(range(GROUPS), key=lambda g: 0 if in_sine_range(g) else 1)
+            w_tiles = dict([(g, load_w_emb(g)) for g in order])
+            for i, vec in enumerate((g0, beta0)):
+                nc.sync.dma_start(
+                    out=vec_bf[:, i], in_=vec.rearrange("(g m t) -> m g t", g=GROUPS, m=P, t=PACK)
+                )
+            timings = dict([(g, timing_sines(g, timing_angles(g))) for g in order[0:T_AHEAD]])
             xT_ps = ps_z.tile([P, TOKENS], BF16, tag="z")
             for b in range(BATCH):
                 nc.tensor.transpose(
@@ -194,10 +203,8 @@ def tile_ffnn_encoder_pa_k_kernel(
             nc.tensor.transpose(out=b_ps[:], in_=b_rows[:], identity=ident_bf[:])
             nc.vector.tensor_copy(out=bias_emb[:], in_=b_ps[:, 0:D_TILES])
 
-            timings = [timing_sines(g, timing_angles(g)) for g in range(2)]
+            nc.gpsimd.memset(w_planes[:].rearrange("p g n -> p (g n)").bitcast(F32), 0.0)
             nc.gpsimd.tensor_copy(out=gain_beta[:], in_=vec_bf[:].rearrange("p v g t -> p v (g t)"))
-
-            nc.vector.memset(w_planes[:].rearrange("p g n -> p (g n)").bitcast(I32), 0)
             for o, (words, scales, bias) in enumerate(weights):
                 cols = slice(o * N_OUT, (o + 1) * N_OUT)
                 for quad in range(4):
@@ -213,16 +220,20 @@ def tile_ffnn_encoder_pa_k_kernel(
             for o, (words, scales, bias) in enumerate(weights):
                 nc.sync.dma_start(out=bias_all[:, o * N_OUT : (o + 1) * N_OUT], in_=bias.partition_broadcast(P))
 
-            for g in range(GROUPS):
+            for k, g in enumerate(order):
+                if k + T_AHEAD < GROUPS:
+                    later = order[k + T_AHEAD]
+                    timings[later] = timing_sines(later, timing_angles(later))
                 banks = [embed(g, b, w_tiles[g]) for b in range(BATCH)]
                 for b in range(BATCH):
                     bias_relu_timing(g, b, banks[b], timings[g])
-                    square(g, b)
-                if g + 2 < GROUPS:
-                    timings.append(timing_sines(g + 2, timing_angles(g + 2)))
+                    if k >= GROUPS - 2:
+                        square(g, b, 1, k - GROUPS // 2 + 1)
+                    elif k % 2 == 1:
+                        square(g, b, 2, k // 2)
             warm = once.tile([P, 1], F32, tag="warm")
             nc.scalar.activation(
-                out=warm[:], in_=timings[GROUPS - 1][:, 0:1], func=ACT.Sqrt, bias=eps_col[:], scale=0.0
+                out=warm[:], in_=timings[order[GROUPS - 1]][:, 0:1], func=ACT.Sqrt, bias=eps_col[:], scale=0.0
             )
 
         total = keep.tile([P, BATCH], F32)

@@ -29,8 +29,9 @@ N_QK = 2 * N_OUT
 SWEEPS = 2
 HALF = BATCH // SWEEPS
 HALF_TOKENS = HALF * SEQ
-PAIRS = GROUPS // 2
-ROUNDS = SWEEPS * PAIRS
+ROUNDS = SWEEPS * GROUPS
+MX_LAG = 3
+NORM_AHEAD = 4
 EPS = 1e-3
 MAX_TIMESCALE = 10000.0
 D_TILES = D // P
@@ -227,10 +228,19 @@ def tile_ffnn_encoder_pa_k_kernel(
                 banks = [embed(g, b, w_tiles[g]) for b in range(BATCH)]
                 for b in range(BATCH):
                     bias_relu_timing(g, b, banks[b], timings[g])
+                    if k == GROUPS - 1:
+                        continue
                     if k >= GROUPS - 2:
                         square(g, b, 1, k - GROUPS // 2 + 1)
                     elif k % 2 == 1:
                         square(g, b, 2, k // 2)
+            for b in range(BATCH):
+                junk_v = once.tile([P, K_PASS], BF16, tag="junk_v")
+                last = e_rows(order[GROUPS - 1], b)
+                nc.vector.scalar_tensor_tensor(
+                    out=junk_v[:], in0=last, scalar=1.0, in1=last,
+                    op0=ALU.mult, op1=ALU.mult, accum_out=sum_sq[:, b, GROUPS // 2 : GROUPS // 2 + 1],
+                )
             warm = once.tile([P, 1], F32, tag="warm")
             nc.scalar.activation(
                 out=warm[:], in_=timings[order[GROUPS - 1]][:, 0:1], func=ACT.Sqrt, bias=eps_col[:], scale=0.0
@@ -260,22 +270,28 @@ def tile_ffnn_encoder_pa_k_kernel(
         with ExitStack() as stage2:
             ps_acc = stage2.enter_context(tc.psum_pool(name="ps_acc", bufs=1))
             ps_turn = stage2.enter_context(tc.psum_pool(name="ps_turn", bufs=4))
-            h_pool = stage2.enter_context(tc.tile_pool(name="h_pool", bufs=2))
-            code_pool = stage2.enter_context(tc.tile_pool(name="code_pool", bufs=3))
+            h_pool = stage2.enter_context(tc.tile_pool(name="h_pool", bufs=3))
+            code_pool = stage2.enter_context(tc.tile_pool(name="code_pool", bufs=MX_LAG + 1))
             out_pool = stage2.enter_context(tc.tile_pool(name="out_pool", bufs=2))
 
-            def groups_of(r):
-                return (2 * (r % PAIRS), 2 * (r % PAIRS) + 1)
+            def group_of(r):
+                return r % GROUPS
 
             def entries_of(r):
-                return tuple(range(HALF * (r // PAIRS), HALF * (r // PAIRS) + HALF))
+                return tuple(range(HALF * (r // GROUPS), HALF * (r // GROUPS) + HALF))
 
-            def normalise(g, b):
-                nc.vector.tensor_scalar(
-                    out=e_rows(g, b), in0=e_rows(g, b),
-                    scalar1=rstd[:, b : b + 1], scalar2=neg_mean_rstd[:, b : b + 1],
-                    op0=ALU.mult, op1=ALU.add,
-                )
+            def normalise(g, b, on_scalar=False):
+                if on_scalar:
+                    nc.scalar.activation(
+                        out=e_rows(g, b), in_=e_rows(g, b), func=ACT.Identity,
+                        bias=neg_mean_rstd[:, b : b + 1], scale=rstd[:, b : b + 1],
+                    )
+                else:
+                    nc.vector.tensor_scalar(
+                        out=e_rows(g, b), in0=e_rows(g, b),
+                        scalar1=rstd[:, b : b + 1], scalar2=neg_mean_rstd[:, b : b + 1],
+                        op0=ALU.mult, op1=ALU.add,
+                    )
 
             def gain_and_beta(g, entries, t_pair, h_slot):
                 turned = ps_turn.tile([P, 2, HALF_TOKENS], F32, tag="turned")
@@ -296,28 +312,26 @@ def tile_ffnn_encoder_pa_k_kernel(
                     )
 
             def regroup(h_T):
-                grouped = h_pool.tile([P, 2, HALF_TOKENS, PACK], BF16, tag="grouped", align_bytes=64)
-                nc.vector.tensor_copy(out=grouped[:], in_=h_T[:].rearrange("p k t w -> p k w t"))
+                grouped = h_pool.tile([P, HALF_TOKENS, PACK], BF16, tag="grouped", align_bytes=64, bufs=2)
+                nc.vector.tensor_copy(out=grouped[:], in_=h_T[:].rearrange("p t w -> p w t"))
                 return grouped
 
             def quantise(grouped):
-                codes = code_pool.tile([P, 2, HALF_TOKENS], U32, tag="codes", align_bytes=64)
-                plane = code_pool.tile([P, 2, HALF_TOKENS], U8, tag="plane", align_bytes=64)
+                codes = code_pool.tile([P, HALF_TOKENS], U32, tag="codes", align_bytes=64)
+                plane = code_pool.tile([P, HALF_TOKENS], U8, tag="plane", align_bytes=64)
                 nc.vector.quantize_mx(
-                    out=codes[:].rearrange("p k w -> p (k w)").bitcast(FP8X4),
-                    scales=plane[:].rearrange("p k w -> p (k w)"),
-                    in_=grouped[:].rearrange("p k w t -> p (k w t)"),
+                    out=codes[:].bitcast(FP8X4), scales=plane[:], in_=grouped[:].rearrange("p w t -> p (w t)")
                 )
                 return codes, plane
 
-            def project(g, k, quantised, acc):
+            def project(g, quantised, acc):
                 for i in range(HALF):
                     tokens = slice(i * SEQ, (i + 1) * SEQ)
                     for bank, cols in ((acc[i][0][:], slice(0, N_QK)), (acc[i][1][:, 0:N_OUT], slice(N_QK, N_ALL))):
                         nc.tensor.matmul_mx(
                             out=bank,
-                            lhsT=quantised[0][:, k, tokens].bitcast(FP8X4),
-                            lhsT_scale=quantised[1][:, k, tokens],
+                            lhsT=quantised[0][:, tokens].bitcast(FP8X4),
+                            lhsT_scale=quantised[1][:, tokens],
                             rhs=w_words[:, g, cols].bitcast(FP8X4),
                             rhs_scale=w_planes[:, g, cols],
                             start=(g == 0),
@@ -336,38 +350,37 @@ def tile_ffnn_encoder_pa_k_kernel(
                     )
                     nc.sync.dma_start(out=outs[2][b], in_=rows_v[:])
 
-            for r in range(2):
-                for g in groups_of(r):
-                    for b in entries_of(r):
-                        normalise(g, b)
+            for r in range(NORM_AHEAD):
+                for b in entries_of(r):
+                    normalise(group_of(r), b)
             h_tiles = {}
             quantised = {}
             acc = None
-            for r in range(ROUNDS + 2):
-                ahead = [(g, b) for g in groups_of(r + 2) for b in entries_of(r + 2)] if r + 2 < ROUNDS else []
+            for r in range(ROUNDS + MX_LAG):
+                ahead = [(group_of(r + NORM_AHEAD), b) for b in entries_of(r + NORM_AHEAD)] if r + NORM_AHEAD < ROUNDS else []
+                behind = r - MX_LAG
                 if r < ROUNDS:
-                    h_T = h_pool.tile([P, 2, PACK, HALF_TOKENS], BF16, tag="h_T")
+                    h_T = h_pool.tile([P, PACK, HALF_TOKENS], BF16, tag="h_T")
                     h_tiles[r] = h_T
-                for k in range(2):
-                    if r < ROUNDS:
-                        for t_pair in range(PACK // 2):
-                            gain_and_beta(groups_of(r)[k], entries_of(r), t_pair, h_tiles[r][:, k])
-                    if 0 <= r - 2:
-                        if k == 0 and (r - 2) % PAIRS == 0:
-                            acc = [
-                                (
-                                    ps_acc.tile([P, N_QK], F32, name="acc_qk%d" % i),
-                                    ps_acc.tile([P, N_QK], F32, name="acc_v%d" % i),
-                                )
-                                for i in range(HALF)
-                            ]
-                        project(groups_of(r - 2)[k], k, quantised[r - 2], acc)
-                    for g, b in ahead[2 * k : 2 * k + 2]:
-                        normalise(g, b)
-                    if 0 <= r - 1 < ROUNDS:
-                        if k == 0:
-                            grouped = regroup(h_tiles[r - 1])
-                        else:
-                            quantised[r - 1] = quantise(grouped)
-                if 0 <= r - 2 and (r - 2) % PAIRS == PAIRS - 1:
-                    store(entries_of(r - 2), acc)
+                    for t_pair in range(PACK // 2):
+                        gain_and_beta(group_of(r), entries_of(r), t_pair, h_tiles[r])
+                if 0 <= behind:
+                    if group_of(behind) == 0:
+                        acc = [
+                            (
+                                ps_acc.tile([P, N_QK], F32, name="acc_qk%d" % i),
+                                ps_acc.tile([P, N_QK], F32, name="acc_v%d" % i),
+                            )
+                            for i in range(HALF)
+                        ]
+                    project(group_of(behind), quantised[behind], acc)
+                for g, b in ahead[0:1]:
+                    normalise(g, b)
+                if 0 <= r - 1 < ROUNDS:
+                    grouped = regroup(h_tiles[r - 1])
+                for g, b in ahead[1:2]:
+                    normalise(g, b, on_scalar=(r % 2 == 1))
+                if 0 <= r - 1 < ROUNDS:
+                    quantised[r - 1] = quantise(grouped)
+                if 0 <= behind and group_of(behind) == GROUPS - 1:
+                    store(entries_of(behind), acc)

@@ -312,7 +312,7 @@ def tile_ffnn_encoder_pa_k_kernel(
                     )
 
             def regroup(h_T):
-                grouped = h_pool.tile([P, HALF_TOKENS, PACK], BF16, tag="grouped", align_bytes=64, bufs=2)
+                grouped = h_pool.tile([P, HALF_TOKENS, PACK], BF16, tag="grouped", align_bytes=64)
                 nc.vector.tensor_copy(out=grouped[:], in_=h_T[:].rearrange("p t w -> p w t"))
                 return grouped
 
@@ -354,6 +354,7 @@ def tile_ffnn_encoder_pa_k_kernel(
                 for b in entries_of(r):
                     normalise(group_of(r), b)
             h_tiles = {}
+            grouped_tiles = {}
             quantised = {}
             acc = None
             for r in range(ROUNDS + MX_LAG):
@@ -374,13 +375,13 @@ def tile_ffnn_encoder_pa_k_kernel(
                             for i in range(HALF)
                         ]
                     project(group_of(behind), quantised[behind], acc)
+                if 0 <= r - 2 < ROUNDS:
+                    quantised[r - 2] = quantise(grouped_tiles[r - 2])
                 for g, b in ahead[0:1]:
                     normalise(g, b)
                 if 0 <= r - 1 < ROUNDS:
-                    grouped = regroup(h_tiles[r - 1])
+                    grouped_tiles[r - 1] = regroup(h_tiles[r - 1])
                 for g, b in ahead[1:2]:
                     normalise(g, b, on_scalar=(r % 2 == 1))
-                if 0 <= r - 1 < ROUNDS:
-                    quantised[r - 1] = quantise(grouped)
                 if 0 <= behind and group_of(behind) == GROUPS - 1:
                     store(entries_of(behind), acc)

import math
from contextlib import ExitStack

import concourse.mybir as mybir
from concourse.masks import make_identity

F32 = mybir.dt.float32
BF16 = mybir.dt.bfloat16
I32 = mybir.dt.int32
U32 = mybir.dt.uint32
U8 = mybir.dt.uint8
FP8X4 = mybir.dt.float8_e4m3fn_x4
ACT = mybir.ActivationFunctionType
ALU = mybir.AluOpType
AXIS = mybir.AxisListType

P = 128
BATCH = 4
SEQ = 128
TOKENS = BATCH * SEQ
D = 8192
PACK = 4
K_PASS = P * PACK
GROUPS = D // K_PASS
SINE_GROUPS = GROUPS // 2
N_OUT = 256
N_ALL = 3 * N_OUT
N_QK = 2 * N_OUT
SWEEPS = 2
HALF = BATCH // SWEEPS
HALF_TOKENS = HALF * SEQ
ROUNDS = SWEEPS * GROUPS
MX_LAG = 3
NORM_AHEAD = 4
EPS = 1e-3
MAX_TIMESCALE = 10000.0
D_TILES = D // P
T_AHEAD = 4

FLOPS = 2 * TOKENS * P * D + 2 * TOKENS * D * N_ALL


def inv_timescale(i):
    return MAX_TIMESCALE ** (-i / (D // 2 - 1.0))


def in_sine_range(g):
    return (SEQ - 1) * inv_timescale(K_PASS * (g % SINE_GROUPS)) + math.pi / 2 <= math.pi


def tile_ffnn_encoder_pa_k_kernel(
    tc, x, W_emb, b_emb, g0, beta0,
    Wq_words, Wq_scales, bq, Wk_words, Wk_scales, bk, Wv_words, Wv_scales, bv,
    out_0, out_1, out_2,
):
    nc = tc.nc
    weights = ((Wq_words, Wq_scales, bq), (Wk_words, Wk_scales, bk), (Wv_words, Wv_scales, bv))
    outs = (out_0, out_1, out_2)

    with ExitStack() as ctx:
        ctx.enter_context(tc.manual_schedule())
        keep = ctx.enter_context(tc.tile_pool(name="keep", bufs=1))

        x_rows = keep.tile([P, BATCH, P], BF16)
        nc.sync.dma_start(out=x_rows[:], in_=x.rearrange("b s f -> s b f"))
        b_rows = keep.tile([P, P], BF16)
        nc.vector.memset(b_rows[:], 0.0)
        nc.sync.dma_start(out=b_rows[0:D_TILES, :], in_=b_emb.rearrange("(c i) -> c i", i=P))
        vec_bf = keep.tile([P, 2, GROUPS, PACK], BF16)

        ident_bf = keep.tile([P, P], BF16)
        make_identity(nc, ident_bf[:])
        pos_i = keep.tile([P, 1], I32)
        nc.gpsimd.iota(pos_i[:], pattern=[[0, 1]], base=0, channel_multiplier=1)
        ident_f32 = keep.tile([P, P], F32)
        make_identity(nc, ident_f32[:])

        w_base = keep.tile([P, K_PASS], F32)
        nc.vector.memset(w_base[:, 0:1], 1.0)
        for bit in range(7):
            n = 1 << bit
            nc.vector.tensor_scalar_mul(
                out=w_base[:, n : 2 * n], in0=w_base[:, 0:n], scalar1=inv_timescale(PACK * n)
            )
        for bit in range(2):
            n = P << bit
            nc.vector.tensor_scalar_mul(
                out=w_base[:, n : 2 * n], in0=w_base[:, 0:n], scalar1=inv_timescale(1 << bit)
            )
        pos_f = keep.tile([P, 1], F32)
        nc.vector.tensor_copy(out=pos_f[:], in_=pos_i[:])
        pos_w = keep.tile([P, SINE_GROUPS], F32)
        for j in range(SINE_GROUPS):
            nc.vector.tensor_scalar_mul(
                out=pos_w[:, j : j + 1], in0=pos_f[:], scalar1=inv_timescale(K_PASS * j)
            )
        zero_col = keep.tile([P, 1], F32)
        nc.vector.memset(zero_col[:], 0.0)
        half_pi = keep.tile([P, 1], F32)
        nc.vector.tensor_scalar_add(out=half_pi[:], in0=zero_col[:], scalar1=math.pi / 2)
        eps_col = keep.tile([P, 1], F32)
        nc.vector.tensor_scalar_add(out=eps_col[:], in0=zero_col[:], scalar1=EPS)

        sum_e = keep.tile([P, BATCH, GROUPS], F32)
        sum_sq = keep.tile([P, BATCH, GROUPS // 2 + 1], F32)
        e_pairs = [keep.tile([P, BATCH, 2 * K_PASS], F32, name="e_pair%d" % i) for i in range(GROUPS // 2)]

        def e_rows(g, b):
            return e_pairs[g // 2][:, b, (g % 2) * K_PASS : (g % 2 + 1) * K_PASS]

        xT = keep.tile([P, TOKENS], BF16)
        w_words = keep.tile([P, GROUPS, N_ALL], U32, align_bytes=64)
        w_planes = keep.tile([P, GROUPS, N_ALL], U8, align_bytes=64)
        bias_all = keep.tile([P, N_ALL], BF16)
        gain_beta = keep.tile([P, 2, GROUPS * PACK], F32)
        bias_emb = keep.tile([P, D_TILES], F32)
        gain, beta = gain_beta[:, 0], gain_beta[:, 1]

        with ExitStack() as stage1:
            ps_z = stage1.enter_context(tc.psum_pool(name="ps_z", bufs=8))
            w_pool = stage1.enter_context(tc.tile_pool(name="w_pool", bufs=GROUPS))
            time_pool = stage1.enter_context(tc.tile_pool(name="time_pool", bufs=T_AHEAD + 1))
            angle_pool = stage1.enter_context(tc.tile_pool(name="angle_pool", bufs=2))
            once = stage1.enter_context(tc.tile_pool(name="once", bufs=1))

            def load_w_emb(g):
                w_cols = w_pool.tile([P, K_PASS], BF16, tag="w_cols")
                nc.sync.dma_start(out=w_cols[:], in_=W_emb[:, g * K_PASS : (g + 1) * K_PASS])
                return w_cols

            def timing_angles(g):
                j = g % SINE_GROUPS
                if in_sine_range(g):
                    return w_base, pos_w[:, j : j + 1]
                angle = angle_pool.tile([P, K_PASS], F32, tag="angle")
                nc.gpsimd.tensor_scalar(
                    out=angle[:], in0=w_base[:], scalar1=pos_w[:, j : j + 1], scalar2=0.0,
                    op0=ALU.mult, op1=ALU.add,
                )
                turns = angle_pool.tile([P, K_PASS], I32, tag="turns")
                nc.gpsimd.tensor_scalar(
                    out=turns[:], in0=angle[:], scalar1=0.5 / math.pi,
                    scalar2=0.25 if g >= SINE_GROUPS else 0.0, op0=ALU.mult, op1=ALU.add,
                )
                nc.vector.scalar_tensor_tensor(
                    out=angle[:], in0=turns[:], scalar=-2.0 * math.pi, in1=angle[:], op0=ALU.mult, op1=ALU.add
                )
                return angle, 1.0

            def timing_sines(g, angles):
                timing = time_pool.tile([P, K_PASS], F32, tag="timing")
                shift = half_pi if g >= SINE_GROUPS else zero_col
                nc.scalar.activation(out=timing[:], in_=angles[0][:], func=ACT.Sin, bias=shift[:], scale=angles[1])
                return timing

            def embed(g, b, w_cols):
                z = ps_z.tile([P, K_PASS], F32, tag="z")
                nc.tensor.matmul(
                    out=z[:], lhsT=xT[:, b * SEQ : (b + 1) * SEQ], rhs=w_cols[:], start=True, stop=False
                )
                return z

            def bias_relu_timing(g, b, z, timing):
                for j in range(PACK):
                    c = g * PACK + j
                    nc.tensor.matmul(
                        out=z[:, j * P : (j + 1) * P],
                        lhsT=bias_emb[:, c : c + 1].to_broadcast([P, P]),
                        rhs=ident_f32[:],
                        is_transpose=True,
                        start=False,
                        stop=(j == PACK - 1),
                    )
                nc.vector.scalar_tensor_tensor(
                    out=e_rows(g, b).rearrange("p (t m) -> p t m", t=PACK),
                    in0=z[:].rearrange("p (m t) -> p t m", t=PACK),
                    scalar=0.0,
                    in1=timing[:].rearrange("p (t m) -> p t m", t=PACK),
                    op0=ALU.max, op1=ALU.add, accum_out=sum_e[:, b, g : g + 1],
                )

            def square(g, b, groups, column):
                first = (g % 2 + 1 - groups) * K_PASS
                junk = once.tile([P, 2 * K_PASS], BF16, tag="junk")
                nc.scalar.activation(
                    out=junk[:, 0 : groups * K_PASS], in_=e_pairs[g // 2][:, b, first : first + groups * K_PASS],
                    func=ACT.Square, accum_out=sum_sq[:, b, column : column + 1],
                )

            order = sorted(range(GROUPS), key=lambda g: 0 if in_sine_range(g) else 1)
            w_tiles = dict([(g, load_w_emb(g)) for g in order])
            for i, vec in enumerate((g0, beta0)):
                nc.sync.dma_start(
                    out=vec_bf[:, i], in_=vec.rearrange("(g m t) -> m g t", g=GROUPS, m=P, t=PACK)
                )
            timings = dict([(g, timing_sines(g, timing_angles(g))) for g in order[0:T_AHEAD]])
            xT_ps = ps_z.tile([P, TOKENS], BF16, tag="z")
            for b in range(BATCH):
                nc.tensor.transpose(
                    out=xT_ps[:, b * SEQ : (b + 1) * SEQ], in_=x_rows[:, b, :], identity=ident_bf[:]
                )
            nc.vector.tensor_copy(out=xT[:], in_=xT_ps[:])
            b_ps = ps_z.tile([P, P], BF16, tag="z")
            nc.tensor.transpose(out=b_ps[:], in_=b_rows[:], identity=ident_bf[:])
            nc.vector.tensor_copy(out=bias_emb[:], in_=b_ps[:, 0:D_TILES])

            nc.gpsimd.memset(w_planes[:].rearrange("p g n -> p (g n)").bitcast(F32), 0.0)
            nc.gpsimd.tensor_copy(out=gain_beta[:], in_=vec_bf[:].rearrange("p v g t -> p v (g t)"))
            for o, (words, scales, bias) in enumerate(weights):
                cols = slice(o * N_OUT, (o + 1) * N_OUT)
                for quad in range(4):
                    nc.sync.dma_start(
                        out=w_planes[32 * quad : 32 * quad + 4, :, cols].bitcast(I32),
                        in_=scales.rearrange("g q n -> q g n")[4 * quad : 4 * quad + 4].bitcast(I32),
                    )
            for o, (words, scales, bias) in enumerate(weights):
                nc.sync.dma_start(
                    out=w_words[:, :, o * N_OUT : (o + 1) * N_OUT].bitcast(I32),
                    in_=words.rearrange("g p n t -> p g (n t)").bitcast(I32),
                )
            for o, (words, scales, bias) in enumerate(weights):
                nc.sync.dma_start(out=bias_all[:, o * N_OUT : (o + 1) * N_OUT], in_=bias.partition_broadcast(P))

            for k, g in enumerate(order):
                if k + T_AHEAD < GROUPS:
                    later = order[k + T_AHEAD]
                    timings[later] = timing_sines(later, timing_angles(later))
                banks = [embed(g, b, w_tiles[g]) for b in range(BATCH)]
                for b in range(BATCH):
                    bias_relu_timing(g, b, banks[b], timings[g])
                    if k == GROUPS - 1:
                        continue
                    if k >= GROUPS - 2:
                        square(g, b, 1, k - GROUPS // 2 + 1)
                    elif k % 2 == 1:
                        square(g, b, 2, k // 2)
            for b in range(BATCH):
                junk_v = once.tile([P, K_PASS], BF16, tag="junk_v")
                last = e_rows(order[GROUPS - 1], b)
                nc.vector.scalar_tensor_tensor(
                    out=junk_v[:], in0=last, scalar=1.0, in1=last,
                    op0=ALU.mult, op1=ALU.mult, accum_out=sum_sq[:, b, GROUPS // 2 : GROUPS // 2 + 1],
                )
            warm = once.tile([P, 1], F32, tag="warm")
            nc.scalar.activation(
                out=warm[:], in_=timings[order[GROUPS - 1]][:, 0:1], func=ACT.Sqrt, bias=eps_col[:], scale=0.0
            )

        total = keep.tile([P, BATCH], F32)
        nc.vector.tensor_reduce(out=total[:], in_=sum_e[:], axis=AXIS.X, op=ALU.add)
        mean = keep.tile([P, BATCH], F32)
        nc.vector.tensor_scalar_mul(out=mean[:], in0=total[:], scalar1=1.0 / D)
        mean_sq = keep.tile([P, BATCH], F32)
        nc.vector.tensor_mul(out=mean_sq[:], in0=mean[:], in1=mean[:])
        sq_sum = keep.tile([P, BATCH], F32)
        nc.vector.tensor_reduce(out=sq_sum[:], in_=sum_sq[:], axis=AXIS.X, op=ALU.add)
        var = keep.tile([P, BATCH], F32)
        nc.vector.scalar_tensor_tensor(
            out=var[:], in0=sq_sum[:], scalar=1.0 / D, in1=mean_sq[:], op0=ALU.mult, op1=ALU.subtract
        )
        std = keep.tile([P, BATCH], F32)
        nc.scalar.activation(out=std[:], in_=var[:], func=ACT.Sqrt, bias=eps_col[:], scale=1.0)
        rstd = keep.tile([P, BATCH], F32)
        nc.vector.reciprocal(out=rstd[:], in_=std[:])
        neg_mean_rstd = keep.tile([P, BATCH], F32)
        nc.vector.scalar_tensor_tensor(
            out=neg_mean_rstd[:], in0=mean[:], scalar=-1.0, in1=rstd[:], op0=ALU.mult, op1=ALU.mult
        )

        with ExitStack() as stage2:
            ps_acc = stage2.enter_context(tc.psum_pool(name="ps_acc", bufs=1))
            ps_turn = stage2.enter_context(tc.psum_pool(name="ps_turn", bufs=4))
            h_pool = stage2.enter_context(tc.tile_pool(name="h_pool", bufs=3))
            code_pool = stage2.enter_context(tc.tile_pool(name="code_pool", bufs=MX_LAG + 1))
            out_pool = stage2.enter_context(tc.tile_pool(name="out_pool", bufs=2))

            def group_of(r):
                return r % GROUPS

            def entries_of(r):
                return tuple(range(HALF * (r // GROUPS), HALF * (r // GROUPS) + HALF))

            def normalise(g, b, on_scalar=False):
                if on_scalar:
                    nc.scalar.activation(
                        out=e_rows(g, b), in_=e_rows(g, b), func=ACT.Identity,
                        bias=neg_mean_rstd[:, b : b + 1], scale=rstd[:, b : b + 1],
                    )
                else:
                    nc.vector.tensor_scalar(
                        out=e_rows(g, b), in0=e_rows(g, b),
                        scalar1=rstd[:, b : b + 1], scalar2=neg_mean_rstd[:, b : b + 1],
                        op0=ALU.mult, op1=ALU.add,
                    )

            def gain_and_beta(g, entries, t_pair, h_slot):
                turned = ps_turn.tile([P, 2, HALF_TOKENS], F32, tag="turned")
                for u in range(2):
                    t = 2 * t_pair + u
                    for i, b in enumerate(entries):
                        nc.tensor.transpose(
                            out=turned[:, u, i * SEQ : (i + 1) * SEQ],
                            in_=e_rows(g, b)[:, t * P : (t + 1) * P],
                            identity=ident_f32[:],
                        )
                for u in range(2):
                    t = 2 * t_pair + u
                    c = g * PACK + t
                    nc.scalar.activation(
                        out=h_slot[:, t, :], in_=turned[:, u, :], func=ACT.Identity,
                        bias=beta[:, c : c + 1], scale=gain[:, c : c + 1],
                    )

            def regroup(h_T):
                grouped = h_pool.tile([P, HALF_TOKENS, PACK], BF16, tag="grouped", align_bytes=64)
                nc.vector.tensor_copy(out=grouped[:], in_=h_T[:].rearrange("p t w -> p w t"))
                return grouped

            def quantise(grouped):
                codes = code_pool.tile([P, HALF_TOKENS], U32, tag="codes", align_bytes=64)
                plane = code_pool.tile([P, HALF_TOKENS], U8, tag="plane", align_bytes=64)
                nc.vector.quantize_mx(
                    out=codes[:].bitcast(FP8X4), scales=plane[:], in_=grouped[:].rearrange("p w t -> p (w t)")
                )
                return codes, plane

            def project(g, quantised, acc):
                for i in range(HALF):
                    tokens = slice(i * SEQ, (i + 1) * SEQ)
                    for bank, cols in ((acc[i][0][:], slice(0, N_QK)), (acc[i][1][:, 0:N_OUT], slice(N_QK, N_ALL))):
                        nc.tensor.matmul_mx(
                            out=bank,
                            lhsT=quantised[0][:, tokens].bitcast(FP8X4),
                            lhsT_scale=quantised[1][:, tokens],
                            rhs=w_words[:, g, cols].bitcast(FP8X4),
                            rhs_scale=w_planes[:, g, cols],
                            start=(g == 0),
                            stop=(g == GROUPS - 1),
                        )

            def store(entries, acc):
                for i, b in enumerate(entries):
                    rows_qk = out_pool.tile([P, N_QK], F32, tag="rows_qk")
                    nc.vector.tensor_tensor(out=rows_qk[:], in0=acc[i][0][:], in1=bias_all[:, 0:N_QK], op=ALU.add)
                    nc.sync.dma_start(out=outs[0][b], in_=rows_qk[:, 0:N_OUT])
                    nc.sync.dma_start(out=outs[1][b], in_=rows_qk[:, N_OUT:N_QK])
                    rows_v = out_pool.tile([P, N_OUT], F32, tag="rows_v")
                    nc.vector.tensor_tensor(
                        out=rows_v[:], in0=acc[i][1][:, 0:N_OUT], in1=bias_all[:, N_QK:N_ALL], op=ALU.add
                    )
                    nc.sync.dma_start(out=outs[2][b], in_=rows_v[:])

            for r in range(NORM_AHEAD):
                for b in entries_of(r):
                    normalise(group_of(r), b)
            h_tiles = {}
            grouped_tiles = {}
            quantised = {}
            acc = None
            for r in range(ROUNDS + MX_LAG):
                ahead = [(group_of(r + NORM_AHEAD), b) for b in entries_of(r + NORM_AHEAD)] if r + NORM_AHEAD < ROUNDS else []
                behind = r - MX_LAG
                if r < ROUNDS:
                    h_T = h_pool.tile([P, PACK, HALF_TOKENS], BF16, tag="h_T")
                    h_tiles[r] = h_T
                    for t_pair in range(PACK // 2):
                        gain_and_beta(group_of(r), entries_of(r), t_pair, h_tiles[r])
                if 0 <= behind:
                    if group_of(behind) == 0:
                        acc = [
                            (
                                ps_acc.tile([P, N_QK], F32, name="acc_qk%d" % i),
                                ps_acc.tile([P, N_QK], F32, name="acc_v%d" % i),
                            )
                            for i in range(HALF)
                        ]
                    project(group_of(behind), quantised[behind], acc)
                if 0 <= r - 2 < ROUNDS:
                    quantised[r - 2] = quantise(grouped_tiles[r - 2])
                for g, b in ahead[0:1]:
                    normalise(g, b)
                if 0 <= r - 1 < ROUNDS:
                    grouped_tiles[r - 1] = regroup(h_tiles[r - 1])
                for g, b in ahead[1:2]:
                    normalise(g, b, on_scalar=(r % 2 == 1))
                if 0 <= behind and group_of(behind) == GROUPS - 1:
                    store(entries_of(behind), acc)
